import numpy as np
import ml_dtypes


def mxq(x, axis, fmt="e4m3"):
    dtype, down = {"e4m3": (ml_dtypes.float8_e4m3fn, 7), "e5m2": (ml_dtypes.float8_e5m2, 14)}[fmt]
    v = np.moveaxis(np.asarray(x, np.float32).astype(ml_dtypes.bfloat16).astype(np.float64), axis, -1)
    blocks = v.reshape(v.shape[:-1] + (-1, 32))
    amax = np.abs(blocks).max(-1, keepdims=True)
    byte = np.maximum(np.where(amax > 0, np.frexp(amax)[1] - 1 + 127, 0) - down, 1)
    scale = np.exp2(byte - 127.0)
    codes = (blocks / scale).astype(np.float32).astype(dtype).astype(np.float64)
    return np.moveaxis((codes * scale).reshape(v.shape), -1, axis)


WIDE = False


def mx_kscale(k):
    if not WIDE:
        return np.ones(k)
    levels = np.array([10, -10, 5, -5, 0])
    a = np.random.permutation(np.resize(levels, k // 512 * 4)).reshape(k // 512, 4)
    idx = np.arange(k)
    return np.exp2(a[idx // 512, idx % 128 // 32])


BF16 = ml_dtypes.bfloat16


def bf(x):
    return np.asarray(x, np.float32).astype(BF16)


def f64(x):
    return np.asarray(x).astype(np.float64)


E2M1 = np.array([0.0, 0.5, 1.0, 1.5, 2.0, 3.0, 4.0, 6.0, -0.0, -0.5, -1.0, -1.5, -2.0, -3.0, -4.0, -6.0])


def pack_weight(w, fmt):
    k, n = w.shape
    w = f64(bf(w)).reshape(k // 32, 32, n)
    amax = np.abs(w).max(1)
    if fmt == "e4m3":
        byte = np.frexp(amax)[1] - 1 + 127 - 7
    else:
        mant, ex = np.frexp(amax / 6.0)
        byte = np.where(mant > 0.5, ex, ex - 1) + 127
    byte = np.clip(np.where(amax > 0, byte, 1), 1, 254)
    scaled = (w * np.exp2(127.0 - byte)[:, None, :]).reshape(k, n).astype(np.float32)
    by_word = np.ascontiguousarray(scaled.reshape(k // 512, 128, 4, n).transpose(0, 1, 3, 2))
    if fmt == "e4m3":
        words = by_word.astype(ml_dtypes.float8_e4m3fn).view(np.uint8)
    else:
        c = by_word.astype(ml_dtypes.float4_e2m1fn).view(np.uint8) & 0xF
        words = c[..., 0::2] | (c[..., 1::2] << 4)
    return np.ascontiguousarray(words), np.ascontiguousarray(byte.astype(np.uint8).reshape(k // 512, 16, n))


def unpack_weight(words, scales, fmt):
    g, p, n, _ = words.shape
    if fmt == "e4m3":
        vals = np.ascontiguousarray(words).view(ml_dtypes.float8_e4m3fn).astype(np.float64)
    else:
        nib = np.empty((g, p, n, 4), np.uint8)
        nib[..., 0::2] = words & 0xF
        nib[..., 1::2] = words >> 4
        vals = E2M1[nib]
    vals = vals * np.repeat(np.exp2(scales.astype(np.float64) - 127.0), 8, axis=1)[..., None]
    return vals.transpose(0, 1, 3, 2).reshape(g * 512, n)


B, D, U = 256, 1024, 1024
KD = 3 * U + D
FMT = "e4m3"


def setup_inputs():
    s = np.ones(KD)
    s[3 * U:] = np.sort(mx_kscale(KD))[::KD // D]

    def gate():
        return pack_weight(np.random.standard_normal((KD, U)) * 1.25 / np.sqrt(KD) / s[:, None], FMT)

    def bias():
        return bf(np.random.standard_normal(U) * 0.5)

    x = bf(np.random.standard_normal((B, D)) * s[3 * U:])
    left_state = bf(np.random.standard_normal((B, U)))
    top_state = bf(np.random.standard_normal((B, U)))
    diagonal_state = bf(np.random.standard_normal((B, U)))
    h_cand = bf(np.tanh(np.random.standard_normal((B, U))))
    w_zi_words, w_zi_scales = gate()
    b_zi = bias()
    w_zl_words, w_zl_scales = gate()
    b_zl = bias()
    w_zt_words, w_zt_scales = gate()
    b_zt = bias()
    w_zd_words, w_zd_scales = gate()
    b_zd = bias()
    return {"x": x,
            "left_state": left_state,
            "top_state": top_state,
            "diagonal_state": diagonal_state,
            "h_cand": h_cand,
            "w_zi_words": w_zi_words, "w_zi_scales": w_zi_scales, "b_zi": b_zi,
            "w_zl_words": w_zl_words, "w_zl_scales": w_zl_scales, "b_zl": b_zl,
            "w_zt_words": w_zt_words, "w_zt_scales": w_zt_scales, "b_zt": b_zt,
            "w_zd_words": w_zd_words, "w_zd_scales": w_zd_scales, "b_zd": b_zd}


def reference(x, left_state, top_state, diagonal_state, h_cand, w_zi_words, w_zi_scales, b_zi, w_zl_words, w_zl_scales, b_zl, w_zt_words, w_zt_scales, b_zt, w_zd_words, w_zd_scales, b_zd):
    left, top, diag = f64(left_state), f64(top_state), f64(diagonal_state)
    q = np.concatenate([left, top, diag, f64(x)], axis=1)
    W = np.concatenate([unpack_weight(w_zi_words, w_zi_scales, FMT), unpack_weight(w_zl_words, w_zl_scales, FMT),
                        unpack_weight(w_zt_words, w_zt_scales, FMT), unpack_weight(w_zd_words, w_zd_scales, FMT)], axis=1)
    b = np.concatenate([f64(b_zi), f64(b_zl), f64(b_zt), f64(b_zd)])
    g = ((mxq(q, 1, "e4m3") @ W) + b).reshape(-1, 4, U)
    e = np.exp(g - g.max(axis=1, keepdims=True))
    z = e / e.sum(axis=1, keepdims=True)
    return z[:, 1] * left + z[:, 2] * top + z[:, 3] * diag + z[:, 0] * f64(h_cand)

@@ -1,0 +1,206 @@
+from contextlib import ExitStack
+
+import concourse.mybir as mybir
+from concourse.masks import make_identity
+
+F32 = mybir.dt.float32
+BF16 = mybir.dt.bfloat16
+I32 = mybir.dt.int32
+U32 = mybir.dt.uint32
+U8 = mybir.dt.uint8
+FP8X4 = mybir.dt.float8_e4m3fn_x4
+ALU = mybir.AluOpType
+ACT = mybir.ActivationFunctionType
+
+P = 128
+PACK = 4
+K_PASS = P * PACK
+BATCH = 256
+UNITS = 1024
+K = 4 * UNITS
+PASSES = K // K_PASS
+ROW_TILES = BATCH // P
+GATES = 4
+CHUNK = 256
+CHUNKS = UNITS // CHUNK
+BANK = 512
+PLANES_PER_TILE = 4
+WEIGHT_BUFS = 12
+
+FLOPS = 2 * BATCH * K * GATES * UNITS
+
+
+def tile_multidimensinalgrucell_pb_kernel(
+    tc,
+    x,
+    left_state,
+    top_state,
+    diagonal_state,
+    h_cand,
+    w_zi_words,
+    w_zi_scales,
+    b_zi,
+    w_zl_words,
+    w_zl_scales,
+    b_zl,
+    w_zt_words,
+    w_zt_scales,
+    b_zt,
+    w_zd_words,
+    w_zd_scales,
+    b_zd,
+    out,
+):
+    nc = tc.nc
+    gate_words = [w_zi_words, w_zl_words, w_zt_words, w_zd_words]
+    gate_scales = [w_zi_scales, w_zl_scales, w_zt_scales, w_zd_scales]
+
+    with ExitStack() as ctx:
+        keep = ctx.enter_context(tc.tile_pool(name="keep", bufs=1))
+        stage = ctx.enter_context(tc.tile_pool(name="stage", bufs=4))
+        weights = ctx.enter_context(tc.tile_pool(name="weights", bufs=WEIGHT_BUFS))
+        work = ctx.enter_context(tc.tile_pool(name="work", bufs=2))
+        psum = ctx.enter_context(tc.psum_pool(name="psum", bufs=8))
+
+        identity = keep.tile([P, P], F32)
+        make_identity(nc, identity[:])
+
+        w_planes = keep.tile([P, GATES, PASSES // PLANES_PER_TILE, UNITS], U8, align_bytes=64)
+        nc.vector.memset(w_planes[:].rearrange("p j a n -> p (j a n)").bitcast(I32), 0)
+
+        bias_rows = keep.tile([P, GATES - 1, UNITS], BF16)
+        nc.vector.memset(bias_rows[:], 0.0)
+        plus_minus = keep.tile([P, P], BF16)
+        nc.vector.memset(plus_minus[:], 0.0)
+        nc.vector.memset(plus_minus[0:32, :], 1.0)
+        nc.vector.memset(plus_minus[32:64, :], -1.0)
+
+        def by_partition(rows):
+            return rows.rearrange("(p m) u -> p m u", m=ROW_TILES)
+
+        blend = keep.tile([P, GATES, ROW_TILES, UNITS], BF16)
+        x_rows = keep.tile([P, ROW_TILES, UNITS], BF16)
+        nc.sync.dma_start(out=blend[:, 1], in_=by_partition(left_state))
+        nc.sync.dma_start(out=blend[:, 2], in_=by_partition(top_state))
+        nc.sync.dma_start(out=blend[:, 3], in_=by_partition(diagonal_state))
+        nc.sync.dma_start(out=x_rows[:], in_=by_partition(x))
+
+        for j, bias in enumerate([b_zl, b_zt, b_zd]):
+            nc.scalar.dma_start(out=bias_rows[0:1, j, :], in_=bias.unsqueeze(0))
+            nc.scalar.dma_start(out=bias_rows[32:33, j, :], in_=b_zi.unsqueeze(0))
+
+        for j in range(GATES):
+            for a in range(PASSES // PLANES_PER_TILE):
+                for quadrant in range(4):
+                    nc.sync.dma_start(
+                        out=w_planes[32 * quadrant : 32 * quadrant + 16, j, a, :].bitcast(I32),
+                        in_=gate_scales[j][
+                            PLANES_PER_TILE * a : PLANES_PER_TILE * (a + 1), 4 * quadrant : 4 * quadrant + 4, :
+                        ].bitcast(I32),
+                    )
+
+        w_piece = []
+        for c in range(CHUNKS):
+            pieces = []
+            for j in range(GATES):
+                piece = weights.tile([P, PASSES, CHUNK], I32, name="piece_%d_%d" % (c, j), tag="piece", align_bytes=64)
+                words = gate_words[j].rearrange("g p n t -> p g (n t)")
+                nc.sync.dma_start(
+                    out=piece[:], in_=words[:, :, PACK * CHUNK * c : PACK * CHUNK * (c + 1)].bitcast(I32)
+                )
+                pieces.append(piece)
+            w_piece.append(pieces)
+            if c == 0:
+                nc.sync.dma_start(out=blend[:, 0], in_=by_partition(h_cand))
+
+        q_codes = keep.tile([P, PASSES, BATCH], U32, align_bytes=64)
+        q_planes = keep.tile([P, PASSES, BATCH], U8, align_bytes=64)
+        q_parts = [blend[:, 1], blend[:, 2], blend[:, 3], x_rows[:]]
+        for g in range(PASSES):
+            part = q_parts[g // 2]
+            first_word = (g % 2) * (K_PASS // 2)
+            flipped = psum.tile([P, 2, BATCH], F32, tag="bank")
+            for u in range(2):
+                for m in range(ROW_TILES):
+                    nc.tensor.transpose(
+                        flipped[:, u, P * m : P * (m + 1)],
+                        part[:, m, :].bitcast(F32)[:, first_word + u : first_word + K_PASS // 2 : 2],
+                        identity[:],
+                    )
+            grouped = stage.tile([P, PACK * BATCH], BF16, align_bytes=64)
+            grouped_words = grouped[:].bitcast(F32).rearrange("p (r u) -> p r u", u=2)
+            if g % 2 == 0:
+                nc.scalar.copy(out=grouped_words, in_=flipped[:].rearrange("p u r -> p r u"))
+            else:
+                nc.vector.tensor_copy(out=grouped_words, in_=flipped[:].rearrange("p u r -> p r u"))
+            nc.vector.quantize_mx(out=q_codes[:, g, :].bitcast(FP8X4), scales=q_planes[:, g, :], in_=grouped[:])
+
+        bias_less_i = keep.tile([P, GATES - 1, UNITS], F32)
+        for j in range(GATES - 1):
+            for half in range(UNITS // BANK):
+                cols = slice(BANK * half, BANK * (half + 1))
+                spread = psum.tile([P, BANK], F32, tag="bank")
+                nc.tensor.matmul(spread[:], lhsT=plus_minus[:], rhs=bias_rows[:, j, cols], start=True, stop=True)
+                nc.scalar.copy(out=bias_less_i[:, j, cols], in_=spread[:])
+
+        out_rows = by_partition(out)
+        for c in range(CHUNKS):
+            cols = slice(CHUNK * c, CHUNK * (c + 1))
+            gates = work.tile([P, GATES, ROW_TILES, CHUNK], F32)
+            for j in range(GATES):
+                acc = psum.tile([P, ROW_TILES, CHUNK], F32, tag="bank")
+                for m in range(ROW_TILES):
+                    rows = slice(P * m, P * (m + 1))
+                    for g in range(PASSES):
+                        offset = 4 * (g % PLANES_PER_TILE)
+                        nc.tensor.matmul_mx(
+                            out=acc[:, m, :],
+                            lhsT=q_codes[:, g, rows].bitcast(FP8X4),
+                            lhsT_scale=q_planes[:, g, rows],
+                            rhs=w_piece[c][j][:, g, :].bitcast(FP8X4),
+                            rhs_scale=w_planes[offset:P, j, g // PLANES_PER_TILE, cols],
+                            start=(g == 0),
+                            stop=(g == PASSES - 1),
+                        )
+                if j == 0:
+                    nc.scalar.copy(out=gates[:, 0], in_=acc[:])
+                else:
+                    nc.vector.tensor_tensor(
+                        out=gates[:, j],
+                        in0=acc[:],
+                        in1=bias_less_i[:, j - 1, cols].unsqueeze(1).to_broadcast([P, ROW_TILES, CHUNK]),
+                        op=ALU.add,
+                    )
+
+            top2 = work.tile([P, 2, ROW_TILES, CHUNK], F32)
+            nc.vector.tensor_tensor(out=top2[:], in0=gates[:, 0:2], in1=gates[:, 2:4], op=ALU.max)
+            top = work.tile([P, ROW_TILES, CHUNK], F32)
+            nc.vector.tensor_tensor(out=top[:], in0=top2[:, 0], in1=top2[:, 1], op=ALU.max)
+            nc.vector.tensor_tensor(
+                out=gates[:],
+                in0=gates[:],
+                in1=top[:].unsqueeze(1).to_broadcast([P, GATES, ROW_TILES, CHUNK]),
+                op=ALU.subtract,
+            )
+            total = psum.tile([P, ROW_TILES, CHUNK], F32, tag="bank")
+            for j in range(GATES):
+                nc.scalar.activation(out=gates[:, j], in_=gates[:, j], func=ACT.Exp)
+                nc.tensor.matmul(
+                    total[:].rearrange("p m u -> p (m u)"),
+                    lhsT=identity[:],
+                    rhs=gates[:, j].rearrange("p m u -> p (m u)"),
+                    start=(j == 0),
+                    stop=(j == GATES - 1),
+                )
+            inverse = work.tile([P, ROW_TILES, CHUNK], F32)
+            nc.scalar.activation(out=inverse[:], in_=total[:], func=ACT.Ln)
+            nc.scalar.activation(out=inverse[:], in_=inverse[:], func=ACT.Exp, scale=-1.0)
+
+            weighted = work.tile([P, GATES, ROW_TILES, CHUNK], F32)
+            nc.vector.tensor_tensor(out=weighted[:], in0=gates[:], in1=blend[:, :, :, cols], op=ALU.mult)
+            mix2 = work.tile([P, 2, ROW_TILES, CHUNK], F32)
+            nc.vector.tensor_tensor(out=mix2[:], in0=weighted[:, 0:2], in1=weighted[:, 2:4], op=ALU.add)
+            result = work.tile([P, ROW_TILES, CHUNK], F32)
+            nc.vector.tensor_tensor(out=result[:], in0=mix2[:, 0], in1=mix2[:, 1], op=ALU.add)
+            nc.vector.tensor_tensor(out=result[:], in0=result[:], in1=inverse[:], op=ALU.mult)
+            nc.scalar.dma_start(out=out_rows[:, :, cols], in_=result[:])

@@ -21,9 +21,9 @@ K = 4 * UNITS
 PASSES = K // K_PASS
 ROW_TILES = BATCH // P
 GATES = 4
-CHUNK = 256
-CHUNKS = UNITS // CHUNK
 BANK = 512
+CHUNK = BANK // ROW_TILES
+CHUNK_WIDTHS = [CHUNK // 2] + [CHUNK] * (UNITS // CHUNK - 1) + [CHUNK // 2]
 PLANES_PER_TILE = 4
 WEIGHT_BUFS = 12
 
@@ -85,11 +85,7 @@ def tile_multidimensinalgrucell_pb_kernel(
         nc.sync.dma_start(out=blend[:, 3], in_=by_partition(diagonal_state))
         nc.sync.dma_start(out=x_rows[:], in_=by_partition(x))
 
-        for j, bias in enumerate([b_zl, b_zt, b_zd]):
-            nc.scalar.dma_start(out=bias_rows[0:1, j, :], in_=bias.unsqueeze(0))
-            nc.scalar.dma_start(out=bias_rows[32:33, j, :], in_=b_zi.unsqueeze(0))
-
-        for j in range(GATES):
+        def load_scales(j):
             for a in range(PASSES // PLANES_PER_TILE):
                 for quadrant in range(4):
                     nc.sync.dma_start(
@@ -99,19 +95,30 @@ def tile_multidimensinalgrucell_pb_kernel(
                         ].bitcast(I32),
                     )
 
+        def load_bias_rows():
+            for j, bias in enumerate([b_zl, b_zt, b_zd]):
+                nc.sync.dma_start(out=bias_rows[0:1, j, :], in_=bias.unsqueeze(0))
+                nc.sync.dma_start(out=bias_rows[32:33, j, :], in_=b_zi.unsqueeze(0))
+
         w_piece = []
-        for c in range(CHUNKS):
+        first_unit = 0
+        for c, width in enumerate(CHUNK_WIDTHS):
             pieces = []
             for j in range(GATES):
-                piece = weights.tile([P, PASSES, CHUNK], I32, name="piece_%d_%d" % (c, j), tag="piece", align_bytes=64)
+                if c == 0:
+                    load_scales(j)
+                piece = weights.tile([P, PASSES, width], I32, name="piece_%d_%d" % (c, j), tag="piece", align_bytes=64)
                 words = gate_words[j].rearrange("g p n t -> p g (n t)")
                 nc.sync.dma_start(
-                    out=piece[:], in_=words[:, :, PACK * CHUNK * c : PACK * CHUNK * (c + 1)].bitcast(I32)
+                    out=piece[:], in_=words[:, :, PACK * first_unit : PACK * (first_unit + width)].bitcast(I32)
                 )
                 pieces.append(piece)
+                if c == 0 and j == 0:
+                    load_bias_rows()
             w_piece.append(pieces)
             if c == 0:
                 nc.sync.dma_start(out=blend[:, 0], in_=by_partition(h_cand))
+            first_unit += width
 
         q_codes = keep.tile([P, PASSES, BATCH], U32, align_bytes=64)
         q_planes = keep.tile([P, PASSES, BATCH], U8, align_bytes=64)
@@ -136,19 +143,29 @@ def tile_multidimensinalgrucell_pb_kernel(
             nc.vector.quantize_mx(out=q_codes[:, g, :].bitcast(FP8X4), scales=q_planes[:, g, :], in_=grouped[:])
 
         bias_less_i = keep.tile([P, GATES - 1, UNITS], F32)
-        for j in range(GATES - 1):
-            for half in range(UNITS // BANK):
-                cols = slice(BANK * half, BANK * (half + 1))
-                spread = psum.tile([P, BANK], F32, tag="bank")
-                nc.tensor.matmul(spread[:], lhsT=plus_minus[:], rhs=bias_rows[:, j, cols], start=True, stop=True)
-                nc.scalar.copy(out=bias_less_i[:, j, cols], in_=spread[:])
+
+        def spread_biases():
+            for j in range(GATES - 1):
+                for half in range(UNITS // BANK):
+                    half_cols = slice(BANK * half, BANK * (half + 1))
+                    spread = psum.tile([P, BANK], F32, tag="bank")
+                    nc.tensor.matmul(
+                        spread[:], lhsT=plus_minus[:], rhs=bias_rows[:, j, half_cols], start=True, stop=True
+                    )
+                    nc.scalar.copy(out=bias_less_i[:, j, half_cols], in_=spread[:])
 
         out_rows = by_partition(out)
-        for c in range(CHUNKS):
-            cols = slice(CHUNK * c, CHUNK * (c + 1))
-            gates = work.tile([P, GATES, ROW_TILES, CHUNK], F32)
+        chunk_cols = []
+        first_unit = 0
+        for width in CHUNK_WIDTHS:
+            chunk_cols.append(slice(first_unit, first_unit + width))
+            first_unit += width
+
+        def logits(c):
+            width = CHUNK_WIDTHS[c]
+            gates = work.tile([P, GATES, ROW_TILES, width], F32, name="gates")
             for j in range(GATES):
-                acc = psum.tile([P, ROW_TILES, CHUNK], F32, tag="bank")
+                acc = psum.tile([P, ROW_TILES, width], F32, tag="bank")
                 for m in range(ROW_TILES):
                     rows = slice(P * m, P * (m + 1))
                     for g in range(PASSES):
@@ -158,49 +175,60 @@ def tile_multidimensinalgrucell_pb_kernel(
                             lhsT=q_codes[:, g, rows].bitcast(FP8X4),
                             lhsT_scale=q_planes[:, g, rows],
                             rhs=w_piece[c][j][:, g, :].bitcast(FP8X4),
-                            rhs_scale=w_planes[offset:P, j, g // PLANES_PER_TILE, cols],
+                            rhs_scale=w_planes[offset:P, j, g // PLANES_PER_TILE, chunk_cols[c]],
                             start=(g == 0),
                             stop=(g == PASSES - 1),
                         )
                 if j == 0:
                     nc.scalar.copy(out=gates[:, 0], in_=acc[:])
+                    if c == 0:
+                        spread_biases()
                 else:
                     nc.vector.tensor_tensor(
                         out=gates[:, j],
                         in0=acc[:],
-                        in1=bias_less_i[:, j - 1, cols].unsqueeze(1).to_broadcast([P, ROW_TILES, CHUNK]),
+                        in1=bias_less_i[:, j - 1, chunk_cols[c]].unsqueeze(1).to_broadcast([P, ROW_TILES, width]),
                         op=ALU.add,
                     )
+            return gates
 
-            top2 = work.tile([P, 2, ROW_TILES, CHUNK], F32)
+        def softmax_blend(c, gates):
+            width = CHUNK_WIDTHS[c]
+            top2 = work.tile([P, 2, ROW_TILES, width], F32, name="top2")
             nc.vector.tensor_tensor(out=top2[:], in0=gates[:, 0:2], in1=gates[:, 2:4], op=ALU.max)
-            top = work.tile([P, ROW_TILES, CHUNK], F32)
+            top = work.tile([P, ROW_TILES, width], F32, name="top")
             nc.vector.tensor_tensor(out=top[:], in0=top2[:, 0], in1=top2[:, 1], op=ALU.max)
-            nc.vector.tensor_tensor(
-                out=gates[:],
-                in0=gates[:],
-                in1=top[:].unsqueeze(1).to_broadcast([P, GATES, ROW_TILES, CHUNK]),
-                op=ALU.subtract,
-            )
-            total = psum.tile([P, ROW_TILES, CHUNK], F32, tag="bank")
             for j in range(GATES):
+                nc.vector.tensor_tensor(out=gates[:, j], in0=gates[:, j], in1=top[:], op=ALU.subtract)
                 nc.scalar.activation(out=gates[:, j], in_=gates[:, j], func=ACT.Exp)
-                nc.tensor.matmul(
-                    total[:].rearrange("p m u -> p (m u)"),
-                    lhsT=identity[:],
-                    rhs=gates[:, j].rearrange("p m u -> p (m u)"),
-                    start=(j == 0),
-                    stop=(j == GATES - 1),
-                )
-            inverse = work.tile([P, ROW_TILES, CHUNK], F32)
-            nc.scalar.activation(out=inverse[:], in_=total[:], func=ACT.Ln)
-            nc.scalar.activation(out=inverse[:], in_=inverse[:], func=ACT.Exp, scale=-1.0)
 
-            weighted = work.tile([P, GATES, ROW_TILES, CHUNK], F32)
-            nc.vector.tensor_tensor(out=weighted[:], in0=gates[:], in1=blend[:, :, :, cols], op=ALU.mult)
-            mix2 = work.tile([P, 2, ROW_TILES, CHUNK], F32)
+            weighted = work.tile([P, GATES, ROW_TILES, width], F32, name="weighted")
+
+            def weigh(j):
+                nc.vector.tensor_tensor(
+                    out=weighted[:, j], in0=gates[:, j], in1=blend[:, j, :, chunk_cols[c]], op=ALU.mult
+                )
+
+            weigh(0)
+            weigh(1)
+            sum2 = work.tile([P, 2, ROW_TILES, width], F32, name="sum2")
+            nc.vector.tensor_tensor(out=sum2[:], in0=gates[:, 0:2], in1=gates[:, 2:4], op=ALU.add)
+            inverse = work.tile([P, ROW_TILES, width], F32, name="inverse")
+            nc.vector.tensor_tensor(out=inverse[:], in0=sum2[:, 0], in1=sum2[:, 1], op=ALU.add)
+            nc.scalar.activation(out=inverse[:], in_=inverse[:], func=ACT.Ln)
+            nc.scalar.activation(out=inverse[:], in_=inverse[:], func=ACT.Exp, scale=-1.0)
+            weigh(2)
+            weigh(3)
+            mix2 = work.tile([P, 2, ROW_TILES, width], F32, name="mix2")
             nc.vector.tensor_tensor(out=mix2[:], in0=weighted[:, 0:2], in1=weighted[:, 2:4], op=ALU.add)
-            result = work.tile([P, ROW_TILES, CHUNK], F32)
-            nc.vector.tensor_tensor(out=result[:], in0=mix2[:, 0], in1=mix2[:, 1], op=ALU.add)
-            nc.vector.tensor_tensor(out=result[:], in0=result[:], in1=inverse[:], op=ALU.mult)
-            nc.scalar.dma_start(out=out_rows[:, :, cols], in_=result[:])
+            mix = work.tile([P, ROW_TILES, width], F32, name="mix")
+            nc.vector.tensor_tensor(out=mix[:], in0=mix2[:, 0], in1=mix2[:, 1], op=ALU.add)
+            return mix, inverse
+
+        gates = logits(0)
+        for c in range(len(CHUNK_WIDTHS)):
+            mix, inverse = softmax_blend(c, gates)
+            if c + 1 < len(CHUNK_WIDTHS):
+                gates = logits(c + 1)
+            nc.vector.tensor_tensor(out=mix[:], in0=mix[:], in1=inverse[:], op=ALU.mult)
+            nc.scalar.dma_start(out=out_rows[:, :, chunk_cols[c]], in_=mix[:])

@@ -21,11 +21,13 @@ K = 4 * UNITS
 PASSES = K // K_PASS
 ROW_TILES = BATCH // P
 GATES = 4
+PAIRS = 2
 BANK = 512
-CHUNK = BANK // ROW_TILES
-CHUNK_WIDTHS = [CHUNK // 2] + [CHUNK] * (UNITS // CHUNK - 1) + [CHUNK // 2]
+HALF = UNITS // 2
+PIECES = ((1, 0, HALF), (0, 0, HALF), (1, HALF, HALF), (0, HALF, HALF // 2), (0, HALF + HALF // 2, HALF // 2))
 PLANES_PER_TILE = 4
-WEIGHT_BUFS = 12
+PASSES_PER_LOAD = 4
+WEIGHT_BUFS = 8
 
 FLOPS = 2 * BATCH * K * GATES * UNITS
 
@@ -74,16 +76,22 @@ def tile_multidimensinalgrucell_pb_kernel(
         nc.vector.memset(plus_minus[:], 0.0)
         nc.vector.memset(plus_minus[0:32, :], 1.0)
         nc.vector.memset(plus_minus[32:64, :], -1.0)
+        halves = keep.tile([P, 2], F32)
+        nc.vector.memset(halves[:, 0:1], -0.5)
+        nc.vector.memset(halves[:, 1:2], 0.5)
 
         def by_partition(rows):
             return rows.rearrange("(p m) u -> p m u", m=ROW_TILES)
 
-        blend = keep.tile([P, GATES, ROW_TILES, UNITS], BF16)
+        states = keep.tile([P, GATES, ROW_TILES, UNITS], BF16)
         x_rows = keep.tile([P, ROW_TILES, UNITS], BF16)
-        nc.sync.dma_start(out=blend[:, 1], in_=by_partition(left_state))
-        nc.sync.dma_start(out=blend[:, 2], in_=by_partition(top_state))
-        nc.sync.dma_start(out=blend[:, 3], in_=by_partition(diagonal_state))
+        nc.sync.dma_start(out=states[:, 1], in_=by_partition(left_state))
+        nc.sync.dma_start(out=states[:, 2], in_=by_partition(top_state))
+        nc.sync.dma_start(out=states[:, 3], in_=by_partition(diagonal_state))
         nc.sync.dma_start(out=x_rows[:], in_=by_partition(x))
+        for j, bias in enumerate([b_zl, b_zt, b_zd]):
+            nc.sync.dma_start(out=bias_rows[0:1, j, :], in_=bias.unsqueeze(0))
+            nc.sync.dma_start(out=bias_rows[32:33, j, :], in_=b_zi.unsqueeze(0))
 
         def load_scales(j):
             for a in range(PASSES // PLANES_PER_TILE):
@@ -95,34 +103,37 @@ def tile_multidimensinalgrucell_pb_kernel(
                         ].bitcast(I32),
                     )
 
-        def load_bias_rows():
-            for j, bias in enumerate([b_zl, b_zt, b_zd]):
-                nc.sync.dma_start(out=bias_rows[0:1, j, :], in_=bias.unsqueeze(0))
-                nc.sync.dma_start(out=bias_rows[32:33, j, :], in_=b_zi.unsqueeze(0))
-
-        w_piece = []
-        first_unit = 0
-        for c, width in enumerate(CHUNK_WIDTHS):
-            pieces = []
-            for j in range(GATES):
-                if c == 0:
+        w_words = []
+        for number, (pair, first_unit, width) in enumerate(PIECES):
+            members = []
+            for member in range(2):
+                j = 2 * pair + member
+                if first_unit == 0:
                     load_scales(j)
-                piece = weights.tile([P, PASSES, width], I32, name="piece_%d_%d" % (c, j), tag="piece", align_bytes=64)
-                words = gate_words[j].rearrange("g p n t -> p g (n t)")
-                nc.sync.dma_start(
-                    out=piece[:], in_=words[:, :, PACK * first_unit : PACK * (first_unit + width)].bitcast(I32)
-                )
-                pieces.append(piece)
-                if c == 0 and j == 0:
-                    load_bias_rows()
-            w_piece.append(pieces)
-            if c == 0:
-                nc.sync.dma_start(out=blend[:, 0], in_=by_partition(h_cand))
-            first_unit += width
+                loads = []
+                for first_pass in range(0, PASSES, PASSES_PER_LOAD):
+                    words = weights.tile(
+                        [P, PASSES_PER_LOAD, width],
+                        I32,
+                        name="words_%d_%d_%d" % (number, member, first_pass),
+                        tag="words",
+                        align_bytes=64,
+                    )
+                    nc.sync.dma_start(
+                        out=words[:],
+                        in_=gate_words[j][first_pass : first_pass + PASSES_PER_LOAD]
+                        .rearrange("g p n t -> p g (n t)")[:, :, PACK * first_unit : PACK * (first_unit + width)]
+                        .bitcast(I32),
+                    )
+                    loads.append(words)
+                members.append(loads)
+            w_words.append(members)
+            if number == 0:
+                nc.sync.dma_start(out=states[:, 0], in_=by_partition(h_cand))
 
         q_codes = keep.tile([P, PASSES, BATCH], U32, align_bytes=64)
         q_planes = keep.tile([P, PASSES, BATCH], U8, align_bytes=64)
-        q_parts = [blend[:, 1], blend[:, 2], blend[:, 3], x_rows[:]]
+        q_parts = [states[:, 1], states[:, 2], states[:, 3], x_rows[:]]
         for g in range(PASSES):
             part = q_parts[g // 2]
             first_word = (g % 2) * (K_PASS // 2)
@@ -135,100 +146,92 @@ def tile_multidimensinalgrucell_pb_kernel(
                         identity[:],
                     )
             grouped = stage.tile([P, PACK * BATCH], BF16, align_bytes=64)
-            grouped_words = grouped[:].bitcast(F32).rearrange("p (r u) -> p r u", u=2)
-            if g % 2 == 0:
-                nc.scalar.copy(out=grouped_words, in_=flipped[:].rearrange("p u r -> p r u"))
-            else:
-                nc.vector.tensor_copy(out=grouped_words, in_=flipped[:].rearrange("p u r -> p r u"))
+            nc.scalar.copy(
+                out=grouped[:].bitcast(F32).rearrange("p (r u) -> p r u", u=2),
+                in_=flipped[:].rearrange("p u r -> p r u"),
+            )
             nc.vector.quantize_mx(out=q_codes[:, g, :].bitcast(FP8X4), scales=q_planes[:, g, :], in_=grouped[:])
 
+        state_gap = keep.tile([P, PAIRS, ROW_TILES, UNITS], F32)
+        for pair in reversed(range(PAIRS)):
+            nc.vector.tensor_tensor(
+                out=state_gap[:, pair], in0=states[:, 2 * pair], in1=states[:, 2 * pair + 1], op=ALU.subtract
+            )
+
         bias_less_i = keep.tile([P, GATES - 1, UNITS], F32)
+        for j in range(GATES - 1):
+            for half in range(UNITS // BANK):
+                half_cols = slice(BANK * half, BANK * (half + 1))
+                spread = psum.tile([P, BANK], F32, tag="bank")
+                nc.tensor.matmul(spread[:], lhsT=plus_minus[:], rhs=bias_rows[:, j, half_cols], start=True, stop=True)
+                nc.scalar.copy(out=bias_less_i[:, j, half_cols], in_=spread[:])
 
-        def spread_biases():
-            for j in range(GATES - 1):
-                for half in range(UNITS // BANK):
-                    half_cols = slice(BANK * half, BANK * (half + 1))
-                    spread = psum.tile([P, BANK], F32, tag="bank")
-                    nc.tensor.matmul(
-                        spread[:], lhsT=plus_minus[:], rhs=bias_rows[:, j, half_cols], start=True, stop=True
-                    )
-                    nc.scalar.copy(out=bias_less_i[:, j, half_cols], in_=spread[:])
-
-        out_rows = by_partition(out)
-        chunk_cols = []
-        first_unit = 0
-        for width in CHUNK_WIDTHS:
-            chunk_cols.append(slice(first_unit, first_unit + width))
-            first_unit += width
-
-        def logits(c):
-            width = CHUNK_WIDTHS[c]
-            gates = work.tile([P, GATES, ROW_TILES, width], F32, name="gates")
-            for j in range(GATES):
-                acc = psum.tile([P, ROW_TILES, width], F32, tag="bank")
-                for m in range(ROW_TILES):
-                    rows = slice(P * m, P * (m + 1))
-                    for g in range(PASSES):
-                        offset = 4 * (g % PLANES_PER_TILE)
-                        nc.tensor.matmul_mx(
-                            out=acc[:, m, :],
-                            lhsT=q_codes[:, g, rows].bitcast(FP8X4),
-                            lhsT_scale=q_planes[:, g, rows],
-                            rhs=w_piece[c][j][:, g, :].bitcast(FP8X4),
-                            rhs_scale=w_planes[offset:P, j, g // PLANES_PER_TILE, chunk_cols[c]],
-                            start=(g == 0),
-                            stop=(g == PASSES - 1),
+        def logits(number):
+            pair, first_unit, width = PIECES[number]
+            cols = slice(first_unit, first_unit + width)
+            tiles_per_bank = BANK // width
+            logit = work.tile([P, 2, ROW_TILES, width], F32, name="logit")
+            for member in range(2):
+                j = 2 * pair + member
+                for first_tile in range(0, ROW_TILES, tiles_per_bank):
+                    acc = psum.tile([P, tiles_per_bank, width], F32, tag="bank")
+                    for i in range(tiles_per_bank):
+                        rows = slice(P * (first_tile + i), P * (first_tile + i + 1))
+                        for g in range(PASSES):
+                            offset = 4 * (g % PLANES_PER_TILE)
+                            nc.tensor.matmul_mx(
+                                out=acc[:, i, :],
+                                lhsT=q_codes[:, g, rows].bitcast(FP8X4),
+                                lhsT_scale=q_planes[:, g, rows],
+                                rhs=w_words[number][member][g // PASSES_PER_LOAD][:, g % PASSES_PER_LOAD, :].bitcast(FP8X4),
+                                rhs_scale=w_planes[offset:P, j, g // PLANES_PER_TILE, cols],
+                                start=(g == 0),
+                                stop=(g == PASSES - 1),
+                            )
+                    if j == 0:
+                        nc.scalar.copy(out=logit[:, member, first_tile : first_tile + tiles_per_bank], in_=acc[:])
+                    else:
+                        nc.vector.tensor_tensor(
+                            out=logit[:, member, first_tile : first_tile + tiles_per_bank],
+                            in0=acc[:],
+                            in1=bias_less_i[:, j - 1, cols].unsqueeze(1).to_broadcast([P, tiles_per_bank, width]),
+                            op=ALU.add,
                         )
-                if j == 0:
-                    nc.scalar.copy(out=gates[:, 0], in_=acc[:])
-                    if c == 0:
-                        spread_biases()
-                else:
-                    nc.vector.tensor_tensor(
-                        out=gates[:, j],
-                        in0=acc[:],
-                        in1=bias_less_i[:, j - 1, chunk_cols[c]].unsqueeze(1).to_broadcast([P, ROW_TILES, width]),
-                        op=ALU.add,
-                    )
-            return gates
+            return logit
 
-        def softmax_blend(c, gates):
-            width = CHUNK_WIDTHS[c]
-            top2 = work.tile([P, 2, ROW_TILES, width], F32, name="top2")
-            nc.vector.tensor_tensor(out=top2[:], in0=gates[:, 0:2], in1=gates[:, 2:4], op=ALU.max)
-            top = work.tile([P, ROW_TILES, width], F32, name="top")
-            nc.vector.tensor_tensor(out=top[:], in0=top2[:, 0], in1=top2[:, 1], op=ALU.max)
-            for j in range(GATES):
-                nc.vector.tensor_tensor(out=gates[:, j], in0=gates[:, j], in1=top[:], op=ALU.subtract)
-                nc.scalar.activation(out=gates[:, j], in_=gates[:, j], func=ACT.Exp)
+        def blend_pair(number, logit):
+            pair, first_unit, width = PIECES[number]
+            cols = slice(first_unit, first_unit + width)
+            shape = [P, ROW_TILES, width]
+            share = work.tile(shape, F32, name="share")
+            nc.vector.tensor_tensor(out=share[:], in0=logit[:, 0], in1=logit[:, 1], op=ALU.subtract)
+            lse = work.tile(shape, F32, name="lse_%d" % pair)
+            nc.vector.tensor_tensor(out=lse[:], in0=logit[:, 0], in1=logit[:, 1], op=ALU.max)
+            nc.scalar.activation(out=share[:], in_=share[:], func=ACT.Sigmoid)
+            ln_larger = work.tile(shape, F32, name="ln_larger")
+            nc.scalar.activation(out=ln_larger[:], in_=share[:], func=ACT.Abs, bias=halves[:, 0:1])
+            nc.scalar.activation(out=ln_larger[:], in_=ln_larger[:], func=ACT.Ln, bias=halves[:, 1:2])
+            mixed = work.tile(shape, F32, name="mixed_%d" % pair)
+            nc.vector.tensor_tensor(out=mixed[:], in0=share[:], in1=state_gap[:, pair, :, cols], op=ALU.mult)
+            nc.vector.tensor_tensor(out=mixed[:], in0=mixed[:], in1=states[:, 2 * pair + 1, :, cols], op=ALU.add)
+            nc.vector.tensor_tensor(out=lse[:], in0=lse[:], in1=ln_larger[:], op=ALU.subtract)
+            return lse, mixed
 
-            weighted = work.tile([P, GATES, ROW_TILES, width], F32, name="weighted")
+        def blend_pairs(first_unit, width, lse_0, mixed_0, lse_1, mixed_1):
+            shape = [P, ROW_TILES, width]
+            pair_share = work.tile(shape, F32, name="pair_share")
+            nc.vector.tensor_tensor(out=pair_share[:], in0=lse_0, in1=lse_1, op=ALU.subtract)
+            nc.scalar.activation(out=pair_share[:], in_=pair_share[:], func=ACT.Sigmoid)
+            result = work.tile(shape, F32, name="result")
+            nc.vector.tensor_tensor(out=result[:], in0=mixed_0, in1=mixed_1, op=ALU.subtract)
+            nc.vector.tensor_tensor(out=result[:], in0=result[:], in1=pair_share[:], op=ALU.mult)
+            nc.vector.tensor_tensor(out=result[:], in0=result[:], in1=mixed_1, op=ALU.add)
+            nc.scalar.dma_start(out=by_partition(out)[:, :, first_unit : first_unit + width], in_=result[:])
 
-            def weigh(j):
-                nc.vector.tensor_tensor(
-                    out=weighted[:, j], in0=gates[:, j], in1=blend[:, j, :, chunk_cols[c]], op=ALU.mult
-                )
-
-            weigh(0)
-            weigh(1)
-            sum2 = work.tile([P, 2, ROW_TILES, width], F32, name="sum2")
-            nc.vector.tensor_tensor(out=sum2[:], in0=gates[:, 0:2], in1=gates[:, 2:4], op=ALU.add)
-            inverse = work.tile([P, ROW_TILES, width], F32, name="inverse")
-            nc.vector.tensor_tensor(out=inverse[:], in0=sum2[:, 0], in1=sum2[:, 1], op=ALU.add)
-            nc.scalar.activation(out=inverse[:], in_=inverse[:], func=ACT.Ln)
-            nc.scalar.activation(out=inverse[:], in_=inverse[:], func=ACT.Exp, scale=-1.0)
-            weigh(2)
-            weigh(3)
-            mix2 = work.tile([P, 2, ROW_TILES, width], F32, name="mix2")
-            nc.vector.tensor_tensor(out=mix2[:], in0=weighted[:, 0:2], in1=weighted[:, 2:4], op=ALU.add)
-            mix = work.tile([P, ROW_TILES, width], F32, name="mix")
-            nc.vector.tensor_tensor(out=mix[:], in0=mix2[:, 0], in1=mix2[:, 1], op=ALU.add)
-            return mix, inverse
-
-        gates = logits(0)
-        for c in range(len(CHUNK_WIDTHS)):
-            mix, inverse = softmax_blend(c, gates)
-            if c + 1 < len(CHUNK_WIDTHS):
-                gates = logits(c + 1)
-            nc.vector.tensor_tensor(out=mix[:], in0=mix[:], in1=inverse[:], op=ALU.mult)
-            nc.scalar.dma_start(out=out_rows[:, :, chunk_cols[c]], in_=mix[:])
+        for number, (pair, first_unit, width) in enumerate(PIECES):
+            lse, mixed = blend_pair(number, logits(number))
+            if pair == 1:
+                lse_1, mixed_1, first_unit_1 = lse, mixed, first_unit
+            else:
+                inside = slice(first_unit - first_unit_1, first_unit - first_unit_1 + width)
+                blend_pairs(first_unit, width, lse[:], mixed[:], lse_1[:, :, inside], mixed_1[:, :, inside])

@@ -26,7 +26,7 @@ BANK = 512
 HALF = UNITS // 2
 PIECES = ((1, 0, HALF), (0, 0, HALF), (1, HALF, HALF), (0, HALF, HALF // 2), (0, HALF + HALF // 2, HALF // 2))
 PLANES_PER_TILE = 4
-PASSES_PER_LOAD = 4
+PASSES_PER_LOAD = PLANES_PER_TILE
 WEIGHT_BUFS = 8
 
 FLOPS = 2 * BATCH * K * GATES * UNITS
@@ -89,29 +89,30 @@ def tile_multidimensinalgrucell_pb_kernel(
         nc.sync.dma_start(out=states[:, 2], in_=by_partition(top_state))
         nc.sync.dma_start(out=states[:, 3], in_=by_partition(diagonal_state))
         nc.sync.dma_start(out=x_rows[:], in_=by_partition(x))
-        for j, bias in enumerate([b_zl, b_zt, b_zd]):
-            nc.sync.dma_start(out=bias_rows[0:1, j, :], in_=bias.unsqueeze(0))
-            nc.sync.dma_start(out=bias_rows[32:33, j, :], in_=b_zi.unsqueeze(0))
 
-        def load_scales(j):
-            for a in range(PASSES // PLANES_PER_TILE):
-                for quadrant in range(4):
-                    nc.sync.dma_start(
-                        out=w_planes[32 * quadrant : 32 * quadrant + 16, j, a, :].bitcast(I32),
-                        in_=gate_scales[j][
-                            PLANES_PER_TILE * a : PLANES_PER_TILE * (a + 1), 4 * quadrant : 4 * quadrant + 4, :
-                        ].bitcast(I32),
-                    )
+        def load_bias_rows():
+            for j, bias in enumerate([b_zl, b_zt, b_zd]):
+                nc.sync.dma_start(out=bias_rows[0:1, j, :], in_=bias.unsqueeze(0))
+                nc.sync.dma_start(out=bias_rows[32:33, j, :], in_=b_zi.unsqueeze(0))
+
+        def load_scales(j, a):
+            for quadrant in range(4):
+                nc.sync.dma_start(
+                    out=w_planes[32 * quadrant : 32 * quadrant + 16, j, a, :].bitcast(I32),
+                    in_=gate_scales[j][
+                        PLANES_PER_TILE * a : PLANES_PER_TILE * (a + 1), 4 * quadrant : 4 * quadrant + 4, :
+                    ].bitcast(I32),
+                )
 
         w_words = []
         for number, (pair, first_unit, width) in enumerate(PIECES):
             members = []
             for member in range(2):
                 j = 2 * pair + member
-                if first_unit == 0:
-                    load_scales(j)
                 loads = []
                 for first_pass in range(0, PASSES, PASSES_PER_LOAD):
+                    if first_unit == 0:
+                        load_scales(j, first_pass // PLANES_PER_TILE)
                     words = weights.tile(
                         [P, PASSES_PER_LOAD, width],
                         I32,
@@ -127,6 +128,8 @@ def tile_multidimensinalgrucell_pb_kernel(
                     )
                     loads.append(words)
                 members.append(loads)
+                if number == 0 and member == 0:
+                    load_bias_rows()
             w_words.append(members)
             if number == 0:
                 nc.sync.dma_start(out=states[:, 0], in_=by_partition(h_cand))

@@ -21,13 +21,17 @@ K = 4 * UNITS
 PASSES = K // K_PASS
 ROW_TILES = BATCH // P
 GATES = 4
-PAIRS = 2
+GATE_I = 0
+GATE_L = 1
+GATE_T = 2
+GATE_D = 3
 BANK = 512
-HALF = UNITS // 2
-PIECES = ((1, 0, HALF), (0, 0, HALF), (1, HALF, HALF), (0, HALF, HALF // 2), (0, HALF + HALF // 2, HALF // 2))
+RANGE = BANK
+RANGES = UNITS // RANGE
+LAST_PIECES = ((0, RANGE), (RANGE, RANGE // 2), (RANGE + RANGE // 2, RANGE // 2))
 PLANES_PER_TILE = 4
-PASSES_PER_LOAD = PLANES_PER_TILE
-WEIGHT_BUFS = 8
+PASSES_PER_LOAD = 4
+WEIGHT_BUFS = 11
 
 FLOPS = 2 * BATCH * K * GATES * UNITS
 
@@ -89,50 +93,50 @@ def tile_multidimensinalgrucell_pb_kernel(
         nc.sync.dma_start(out=states[:, 2], in_=by_partition(top_state))
         nc.sync.dma_start(out=states[:, 3], in_=by_partition(diagonal_state))
         nc.sync.dma_start(out=x_rows[:], in_=by_partition(x))
+        for j, bias in enumerate([b_zl, b_zt, b_zd]):
+            nc.sync.dma_start(out=bias_rows[0:1, j, :], in_=bias.unsqueeze(0))
+            nc.sync.dma_start(out=bias_rows[32:33, j, :], in_=b_zi.unsqueeze(0))
 
-        def load_bias_rows():
-            for j, bias in enumerate([b_zl, b_zt, b_zd]):
-                nc.sync.dma_start(out=bias_rows[0:1, j, :], in_=bias.unsqueeze(0))
-                nc.sync.dma_start(out=bias_rows[32:33, j, :], in_=b_zi.unsqueeze(0))
-
-        def load_scales(j, a):
-            for quadrant in range(4):
-                nc.sync.dma_start(
-                    out=w_planes[32 * quadrant : 32 * quadrant + 16, j, a, :].bitcast(I32),
-                    in_=gate_scales[j][
-                        PLANES_PER_TILE * a : PLANES_PER_TILE * (a + 1), 4 * quadrant : 4 * quadrant + 4, :
-                    ].bitcast(I32),
-                )
-
-        w_words = []
-        for number, (pair, first_unit, width) in enumerate(PIECES):
-            members = []
-            for member in range(2):
-                j = 2 * pair + member
-                loads = []
-                for first_pass in range(0, PASSES, PASSES_PER_LOAD):
-                    if first_unit == 0:
-                        load_scales(j, first_pass // PLANES_PER_TILE)
-                    words = weights.tile(
-                        [P, PASSES_PER_LOAD, width],
-                        I32,
-                        name="words_%d_%d_%d" % (number, member, first_pass),
-                        tag="words",
-                        align_bytes=64,
-                    )
+        def load_scales(j):
+            for a in range(PASSES // PLANES_PER_TILE):
+                for quadrant in range(4):
                     nc.sync.dma_start(
-                        out=words[:],
-                        in_=gate_words[j][first_pass : first_pass + PASSES_PER_LOAD]
-                        .rearrange("g p n t -> p g (n t)")[:, :, PACK * first_unit : PACK * (first_unit + width)]
-                        .bitcast(I32),
+                        out=w_planes[32 * quadrant : 32 * quadrant + 16, j, a, :].bitcast(I32),
+                        in_=gate_scales[j][
+                            PLANES_PER_TILE * a : PLANES_PER_TILE * (a + 1), 4 * quadrant : 4 * quadrant + 4, :
+                        ].bitcast(I32),
                     )
-                    loads.append(words)
-                members.append(loads)
-                if number == 0 and member == 0:
-                    load_bias_rows()
-            w_words.append(members)
-            if number == 0:
-                nc.sync.dma_start(out=states[:, 0], in_=by_partition(h_cand))
+
+        def load_words(j, first_unit, width):
+            loads = []
+            for first_pass in range(0, PASSES, PASSES_PER_LOAD):
+                words = weights.tile(
+                    [P, PASSES_PER_LOAD, width],
+                    I32,
+                    name="words_%d_%d_%d" % (j, first_unit, first_pass),
+                    tag="words",
+                    align_bytes=64,
+                )
+                nc.sync.dma_start(
+                    out=words[:],
+                    in_=gate_words[j][first_pass : first_pass + PASSES_PER_LOAD]
+                    .rearrange("g p n t -> p g (n t)")[:, :, PACK * first_unit : PACK * (first_unit + width)]
+                    .bitcast(I32),
+                )
+                loads.append(words)
+            return loads
+
+        w_words = {}
+        for r in range(RANGES):
+            for j in (GATE_T, GATE_D, GATE_L):
+                if r == 0:
+                    load_scales(j)
+                w_words[(j, RANGE * r)] = load_words(j, RANGE * r, RANGE)
+            if r == 0:
+                nc.sync.dma_start(out=states[:, GATE_I], in_=by_partition(h_cand))
+        load_scales(GATE_I)
+        for first_unit, width in LAST_PIECES:
+            w_words[(GATE_I, first_unit)] = load_words(GATE_I, first_unit, width)
 
         q_codes = keep.tile([P, PASSES, BATCH], U32, align_bytes=64)
         q_planes = keep.tile([P, PASSES, BATCH], U8, align_bytes=64)
@@ -155,11 +159,8 @@ def tile_multidimensinalgrucell_pb_kernel(
             )
             nc.vector.quantize_mx(out=q_codes[:, g, :].bitcast(FP8X4), scales=q_planes[:, g, :], in_=grouped[:])
 
-        state_gap = keep.tile([P, PAIRS, ROW_TILES, UNITS], F32)
-        for pair in reversed(range(PAIRS)):
-            nc.vector.tensor_tensor(
-                out=state_gap[:, pair], in0=states[:, 2 * pair], in1=states[:, 2 * pair + 1], op=ALU.subtract
-            )
+        state_gap = keep.tile([P, ROW_TILES, UNITS], F32)
+        nc.vector.tensor_tensor(out=state_gap[:], in0=states[:, GATE_T], in1=states[:, GATE_D], op=ALU.subtract)
 
         bias_less_i = keep.tile([P, GATES - 1, UNITS], F32)
         for j in range(GATES - 1):
@@ -169,72 +170,86 @@ def tile_multidimensinalgrucell_pb_kernel(
                 nc.tensor.matmul(spread[:], lhsT=plus_minus[:], rhs=bias_rows[:, j, half_cols], start=True, stop=True)
                 nc.scalar.copy(out=bias_less_i[:, j, half_cols], in_=spread[:])
 
-        def logits(number):
-            pair, first_unit, width = PIECES[number]
-            cols = slice(first_unit, first_unit + width)
+        def multiply(j, first_unit, width):
             tiles_per_bank = BANK // width
-            logit = work.tile([P, 2, ROW_TILES, width], F32, name="logit")
-            for member in range(2):
-                j = 2 * pair + member
-                for first_tile in range(0, ROW_TILES, tiles_per_bank):
-                    acc = psum.tile([P, tiles_per_bank, width], F32, tag="bank")
-                    for i in range(tiles_per_bank):
-                        rows = slice(P * (first_tile + i), P * (first_tile + i + 1))
-                        for g in range(PASSES):
-                            offset = 4 * (g % PLANES_PER_TILE)
-                            nc.tensor.matmul_mx(
-                                out=acc[:, i, :],
-                                lhsT=q_codes[:, g, rows].bitcast(FP8X4),
-                                lhsT_scale=q_planes[:, g, rows],
-                                rhs=w_words[number][member][g // PASSES_PER_LOAD][:, g % PASSES_PER_LOAD, :].bitcast(FP8X4),
-                                rhs_scale=w_planes[offset:P, j, g // PLANES_PER_TILE, cols],
-                                start=(g == 0),
-                                stop=(g == PASSES - 1),
-                            )
-                    if j == 0:
-                        nc.scalar.copy(out=logit[:, member, first_tile : first_tile + tiles_per_bank], in_=acc[:])
-                    else:
-                        nc.vector.tensor_tensor(
-                            out=logit[:, member, first_tile : first_tile + tiles_per_bank],
-                            in0=acc[:],
-                            in1=bias_less_i[:, j - 1, cols].unsqueeze(1).to_broadcast([P, tiles_per_bank, width]),
-                            op=ALU.add,
+            banks = []
+            for first_tile in range(0, ROW_TILES, tiles_per_bank):
+                acc = psum.tile([P, tiles_per_bank, width], F32, tag="bank")
+                for i in range(tiles_per_bank):
+                    rows = slice(P * (first_tile + i), P * (first_tile + i + 1))
+                    for g in range(PASSES):
+                        offset = 4 * (g % PLANES_PER_TILE)
+                        nc.tensor.matmul_mx(
+                            out=acc[:, i, :],
+                            lhsT=q_codes[:, g, rows].bitcast(FP8X4),
+                            lhsT_scale=q_planes[:, g, rows],
+                            rhs=w_words[(j, first_unit)][g // PASSES_PER_LOAD][:, g % PASSES_PER_LOAD, :].bitcast(FP8X4),
+                            rhs_scale=w_planes[offset:P, j, g // PLANES_PER_TILE, first_unit : first_unit + width],
+                            start=(g == 0),
+                            stop=(g == PASSES - 1),
                         )
+                banks.append((first_tile, tiles_per_bank, acc))
+            return banks
+
+        def logits(j, r):
+            cols = slice(RANGE * r, RANGE * (r + 1))
+            logit = work.tile([P, ROW_TILES, RANGE], F32, name="logit", bufs=3)
+            for first_tile, tiles, acc in multiply(j, RANGE * r, RANGE):
+                nc.vector.tensor_tensor(
+                    out=logit[:, first_tile : first_tile + tiles],
+                    in0=acc[:],
+                    in1=bias_less_i[:, j - 1, cols].unsqueeze(1).to_broadcast([P, tiles, RANGE]),
+                    op=ALU.add,
+                )
             return logit
 
-        def blend_pair(number, logit):
-            pair, first_unit, width = PIECES[number]
-            cols = slice(first_unit, first_unit + width)
-            shape = [P, ROW_TILES, width]
-            share = work.tile(shape, F32, name="share")
-            nc.vector.tensor_tensor(out=share[:], in0=logit[:, 0], in1=logit[:, 1], op=ALU.subtract)
-            lse = work.tile(shape, F32, name="lse_%d" % pair)
-            nc.vector.tensor_tensor(out=lse[:], in0=logit[:, 0], in1=logit[:, 1], op=ALU.max)
+        def join_logits(a, b, name):
+            share = work.tile([P, ROW_TILES, RANGE], F32, name="share")
+            nc.vector.tensor_tensor(out=share[:], in0=a[:], in1=b[:], op=ALU.subtract)
+            lse = work.tile([P, ROW_TILES, RANGE], F32, name=name)
+            nc.vector.tensor_tensor(out=lse[:], in0=a[:], in1=b[:], op=ALU.max)
             nc.scalar.activation(out=share[:], in_=share[:], func=ACT.Sigmoid)
-            ln_larger = work.tile(shape, F32, name="ln_larger")
+            ln_larger = work.tile([P, ROW_TILES, RANGE], F32, name="ln_larger")
             nc.scalar.activation(out=ln_larger[:], in_=share[:], func=ACT.Abs, bias=halves[:, 0:1])
             nc.scalar.activation(out=ln_larger[:], in_=ln_larger[:], func=ACT.Ln, bias=halves[:, 1:2])
-            mixed = work.tile(shape, F32, name="mixed_%d" % pair)
-            nc.vector.tensor_tensor(out=mixed[:], in0=share[:], in1=state_gap[:, pair, :, cols], op=ALU.mult)
-            nc.vector.tensor_tensor(out=mixed[:], in0=mixed[:], in1=states[:, 2 * pair + 1, :, cols], op=ALU.add)
+            return share, lse, ln_larger
+
+        lse_of_three = []
+        gap_to_h_cand = []
+        for r in range(RANGES):
+            cols = slice(RANGE * r, RANGE * (r + 1))
+            logit_t = logits(GATE_T, r)
+            logit_d = logits(GATE_D, r)
+            share, lse, ln_larger = join_logits(logit_t, logit_d, "lse_of_two")
+            mixed = work.tile([P, ROW_TILES, RANGE], F32, name="mixed")
+            nc.vector.tensor_tensor(out=mixed[:], in0=share[:], in1=state_gap[:, :, cols], op=ALU.mult)
+            nc.vector.tensor_tensor(out=mixed[:], in0=mixed[:], in1=states[:, GATE_D, :, cols], op=ALU.add)
             nc.vector.tensor_tensor(out=lse[:], in0=lse[:], in1=ln_larger[:], op=ALU.subtract)
-            return lse, mixed
+            logit_l = logits(GATE_L, r)
+            nc.vector.tensor_tensor(out=mixed[:], in0=mixed[:], in1=states[:, GATE_L, :, cols], op=ALU.subtract)
+            share, lse, ln_larger = join_logits(lse, logit_l, "lse_of_three")
+            nc.vector.tensor_tensor(out=mixed[:], in0=mixed[:], in1=share[:], op=ALU.mult)
+            nc.vector.tensor_tensor(out=mixed[:], in0=mixed[:], in1=states[:, GATE_L, :, cols], op=ALU.add)
+            nc.vector.tensor_tensor(out=lse[:], in0=lse[:], in1=ln_larger[:], op=ALU.subtract)
+            nc.vector.tensor_tensor(out=mixed[:], in0=mixed[:], in1=states[:, GATE_I, :, cols], op=ALU.subtract)
+            lse_of_three.append(lse)
+            gap_to_h_cand.append(mixed)
 
-        def blend_pairs(first_unit, width, lse_0, mixed_0, lse_1, mixed_1):
-            shape = [P, ROW_TILES, width]
-            pair_share = work.tile(shape, F32, name="pair_share")
-            nc.vector.tensor_tensor(out=pair_share[:], in0=lse_0, in1=lse_1, op=ALU.subtract)
-            nc.scalar.activation(out=pair_share[:], in_=pair_share[:], func=ACT.Sigmoid)
-            result = work.tile(shape, F32, name="result")
-            nc.vector.tensor_tensor(out=result[:], in0=mixed_0, in1=mixed_1, op=ALU.subtract)
-            nc.vector.tensor_tensor(out=result[:], in0=result[:], in1=pair_share[:], op=ALU.mult)
-            nc.vector.tensor_tensor(out=result[:], in0=result[:], in1=mixed_1, op=ALU.add)
+        for first_unit, width in LAST_PIECES:
+            r = first_unit // RANGE
+            inside = slice(first_unit - RANGE * r, first_unit - RANGE * r + width)
+            share = work.tile([P, ROW_TILES, width], F32, name="last_share")
+            for first_tile, tiles, acc in multiply(GATE_I, first_unit, width):
+                nc.vector.tensor_tensor(
+                    out=share[:, first_tile : first_tile + tiles],
+                    in0=lse_of_three[r][:, first_tile : first_tile + tiles, inside],
+                    in1=acc[:],
+                    op=ALU.subtract,
+                )
+            nc.scalar.activation(out=share[:], in_=share[:], func=ACT.Sigmoid)
+            result = work.tile([P, ROW_TILES, width], F32, name="result")
+            nc.vector.tensor_tensor(out=result[:], in0=gap_to_h_cand[r][:, :, inside], in1=share[:], op=ALU.mult)
+            nc.vector.tensor_tensor(
+                out=result[:], in0=result[:], in1=states[:, GATE_I, :, first_unit : first_unit + width], op=ALU.add
+            )
             nc.scalar.dma_start(out=by_partition(out)[:, :, first_unit : first_unit + width], in_=result[:])
-
-        for number, (pair, first_unit, width) in enumerate(PIECES):
-            lse, mixed = blend_pair(number, logits(number))
-            if pair == 1:
-                lse_1, mixed_1, first_unit_1 = lse, mixed, first_unit
-            else:
-                inside = slice(first_unit - first_unit_1, first_unit - first_unit_1 + width)
-                blend_pairs(first_unit, width, lse[:], mixed[:], lse_1[:, :, inside], mixed_1[:, :, inside])

@@ -33,6 +33,8 @@ PLANES_PER_TILE = 4
 PASSES_PER_LOAD = 4
 WEIGHT_BUFS = 11
 
+SPLIT = True
+
 FLOPS = 2 * BATCH * K * GATES * UNITS
 
 
@@ -83,6 +85,8 @@ def tile_multidimensinalgrucell_pb_kernel(
         halves = keep.tile([P, 2], F32)
         nc.vector.memset(halves[:, 0:1], -0.5)
         nc.vector.memset(halves[:, 1:2], 0.5)
+        warm = keep.tile([P, 1], F32)
+        nc.scalar.activation(out=warm[:], in_=halves[:, 0:1], func=ACT.Sigmoid)
 
         def by_partition(rows):
             return rows.rearrange("(p m) u -> p m u", m=ROW_TILES)
@@ -132,8 +136,8 @@ def tile_multidimensinalgrucell_pb_kernel(
                 if r == 0:
                     load_scales(j)
                 w_words[(j, RANGE * r)] = load_words(j, RANGE * r, RANGE)
-            if r == 0:
-                nc.sync.dma_start(out=states[:, GATE_I], in_=by_partition(h_cand))
+                if r == 0 and j == GATE_T:
+                    nc.sync.dma_start(out=states[:, GATE_I], in_=by_partition(h_cand))
         load_scales(GATE_I)
         for first_unit, width in LAST_PIECES:
             w_words[(GATE_I, first_unit)] = load_words(GATE_I, first_unit, width)
@@ -159,8 +163,12 @@ def tile_multidimensinalgrucell_pb_kernel(
             )
             nc.vector.quantize_mx(out=q_codes[:, g, :].bitcast(FP8X4), scales=q_planes[:, g, :], in_=grouped[:])
 
-        state_gap = keep.tile([P, ROW_TILES, UNITS], F32)
-        nc.vector.tensor_tensor(out=state_gap[:], in0=states[:, GATE_T], in1=states[:, GATE_D], op=ALU.subtract)
+        gap_td = keep.tile([P, ROW_TILES, UNITS], F32)
+        gap_dl = keep.tile([P, ROW_TILES, UNITS], F32)
+        gap_lh = keep.tile([P, ROW_TILES, UNITS], F32)
+        nc.vector.tensor_tensor(out=gap_td[:], in0=states[:, GATE_T], in1=states[:, GATE_D], op=ALU.subtract)
+        nc.vector.tensor_tensor(out=gap_dl[:], in0=states[:, GATE_D], in1=states[:, GATE_L], op=ALU.subtract)
+        nc.vector.tensor_tensor(out=gap_lh[:], in0=states[:, GATE_L], in1=states[:, GATE_I], op=ALU.subtract)
 
         bias_less_i = keep.tile([P, GATES - 1, UNITS], F32)
         for j in range(GATES - 1):
@@ -191,6 +199,8 @@ def tile_multidimensinalgrucell_pb_kernel(
                 banks.append((first_tile, tiles_per_bank, acc))
             return banks
 
+        TILES = tuple(range(ROW_TILES)) if SPLIT else (slice(0, ROW_TILES),)
+
         def logits(j, r):
             cols = slice(RANGE * r, RANGE * (r + 1))
             logit = work.tile([P, ROW_TILES, RANGE], F32, name="logit", bufs=3)
@@ -205,51 +215,62 @@ def tile_multidimensinalgrucell_pb_kernel(
 
         def join_logits(a, b, name):
             share = work.tile([P, ROW_TILES, RANGE], F32, name="share")
-            nc.vector.tensor_tensor(out=share[:], in0=a[:], in1=b[:], op=ALU.subtract)
-            lse = work.tile([P, ROW_TILES, RANGE], F32, name=name)
-            nc.vector.tensor_tensor(out=lse[:], in0=a[:], in1=b[:], op=ALU.max)
-            nc.scalar.activation(out=share[:], in_=share[:], func=ACT.Sigmoid)
+            larger = work.tile([P, ROW_TILES, RANGE], F32, name=name)
             ln_larger = work.tile([P, ROW_TILES, RANGE], F32, name="ln_larger")
-            nc.scalar.activation(out=ln_larger[:], in_=share[:], func=ACT.Abs, bias=halves[:, 0:1])
-            nc.scalar.activation(out=ln_larger[:], in_=ln_larger[:], func=ACT.Ln, bias=halves[:, 1:2])
-            return share, lse, ln_larger
+            for m in TILES:
+                nc.vector.tensor_tensor(out=share[:, m], in0=a[:, m], in1=b[:, m], op=ALU.subtract)
+            for m in TILES:
+                nc.vector.tensor_tensor(out=larger[:, m], in0=a[:, m], in1=b[:, m], op=ALU.max)
+            for m in TILES:
+                nc.scalar.activation(out=share[:, m], in_=share[:, m], func=ACT.Sigmoid)
+            for m in TILES:
+                nc.scalar.activation(out=ln_larger[:, m], in_=share[:, m], func=ACT.Abs, bias=halves[:, 0:1])
+            for m in TILES:
+                nc.scalar.activation(out=ln_larger[:, m], in_=ln_larger[:, m], func=ACT.Ln, bias=halves[:, 1:2])
+            return share, larger, ln_larger
+
+        def both(out, in0, in1, op):
+            for m in TILES:
+                nc.vector.tensor_tensor(out=out[:, m], in0=in0[:, m], in1=in1[:, m], op=op)
 
         lse_of_three = []
-        gap_to_h_cand = []
+        blends = []
         for r in range(RANGES):
             cols = slice(RANGE * r, RANGE * (r + 1))
             logit_t = logits(GATE_T, r)
             logit_d = logits(GATE_D, r)
             share, lse, ln_larger = join_logits(logit_t, logit_d, "lse_of_two")
-            mixed = work.tile([P, ROW_TILES, RANGE], F32, name="mixed")
-            nc.vector.tensor_tensor(out=mixed[:], in0=share[:], in1=state_gap[:, :, cols], op=ALU.mult)
-            nc.vector.tensor_tensor(out=mixed[:], in0=mixed[:], in1=states[:, GATE_D, :, cols], op=ALU.add)
-            nc.vector.tensor_tensor(out=lse[:], in0=lse[:], in1=ln_larger[:], op=ALU.subtract)
+            blend = work.tile([P, ROW_TILES, RANGE], F32, name="blend")
+            both(blend, share, gap_td[:, :, cols], ALU.mult)
+            both(blend, blend, gap_dl[:, :, cols], ALU.add)
             logit_l = logits(GATE_L, r)
-            nc.vector.tensor_tensor(out=mixed[:], in0=mixed[:], in1=states[:, GATE_L, :, cols], op=ALU.subtract)
+            both(lse, lse, ln_larger, ALU.subtract)
             share, lse, ln_larger = join_logits(lse, logit_l, "lse_of_three")
-            nc.vector.tensor_tensor(out=mixed[:], in0=mixed[:], in1=share[:], op=ALU.mult)
-            nc.vector.tensor_tensor(out=mixed[:], in0=mixed[:], in1=states[:, GATE_L, :, cols], op=ALU.add)
-            nc.vector.tensor_tensor(out=lse[:], in0=lse[:], in1=ln_larger[:], op=ALU.subtract)
-            nc.vector.tensor_tensor(out=mixed[:], in0=mixed[:], in1=states[:, GATE_I, :, cols], op=ALU.subtract)
+            both(blend, blend, share, ALU.mult)
+            both(blend, blend, gap_lh[:, :, cols], ALU.add)
+            both(lse, lse, ln_larger, ALU.subtract)
             lse_of_three.append(lse)
-            gap_to_h_cand.append(mixed)
+            blends.append(blend)
 
         for first_unit, width in LAST_PIECES:
             r = first_unit // RANGE
             inside = slice(first_unit - RANGE * r, first_unit - RANGE * r + width)
-            share = work.tile([P, ROW_TILES, width], F32, name="last_share")
+            share = work.tile([P, ROW_TILES, width], F32, name="share")
+            parts = []
             for first_tile, tiles, acc in multiply(GATE_I, first_unit, width):
+                part = slice(first_tile, first_tile + tiles)
+                parts.append(part)
+                nc.vector.tensor_tensor(out=share[:, part], in0=lse_of_three[r][:, part, inside], in1=acc[:], op=ALU.subtract)
+            for part in parts:
+                nc.scalar.activation(out=share[:, part], in_=share[:, part], func=ACT.Sigmoid)
+            result = blends[r]
+            for part in parts:
+                nc.vector.tensor_tensor(out=result[:, part, inside], in0=result[:, part, inside], in1=share[:, part], op=ALU.mult)
+            for part in parts:
                 nc.vector.tensor_tensor(
-                    out=share[:, first_tile : first_tile + tiles],
-                    in0=lse_of_three[r][:, first_tile : first_tile + tiles, inside],
-                    in1=acc[:],
-                    op=ALU.subtract,
+                    out=result[:, part, inside],
+                    in0=result[:, part, inside],
+                    in1=states[:, GATE_I, part, first_unit : first_unit + width],
+                    op=ALU.add,
                 )
-            nc.scalar.activation(out=share[:], in_=share[:], func=ACT.Sigmoid)
-            result = work.tile([P, ROW_TILES, width], F32, name="result")
-            nc.vector.tensor_tensor(out=result[:], in0=gap_to_h_cand[r][:, :, inside], in1=share[:], op=ALU.mult)
-            nc.vector.tensor_tensor(
-                out=result[:], in0=result[:], in1=states[:, GATE_I, :, first_unit : first_unit + width], op=ALU.add
-            )
-            nc.scalar.dma_start(out=by_partition(out)[:, :, first_unit : first_unit + width], in_=result[:])
+            nc.scalar.dma_start(out=by_partition(out)[:, :, first_unit : first_unit + width], in_=result[:, :, inside])

@@ -33,6 +33,7 @@ PLANES_PER_TILE = 4
 PASSES_PER_LOAD = 4
 WEIGHT_BUFS = 11
 
+SMALL_AFTER = (2, 2, 2, 2, 4, 4, 4, 4, 4, 2, 2, 2, 2)
 SPLIT = True
 
 FLOPS = 2 * BATCH * K * GATES * UNITS
@@ -74,14 +75,16 @@ def tile_multidimensinalgrucell_pb_kernel(
         make_identity(nc, identity[:])
 
         w_planes = keep.tile([P, GATES, PASSES // PLANES_PER_TILE, UNITS], U8, align_bytes=64)
-        nc.vector.memset(w_planes[:].rearrange("p j a n -> p (j a n)").bitcast(I32), 0)
+        for j in (GATE_T, GATE_D, GATE_L, GATE_I):
+            nc.vector.memset(w_planes[:, j].rearrange("p a n -> p (a n)").bitcast(I32), 0)
 
-        bias_rows = keep.tile([P, GATES - 1, UNITS], BF16)
+        bias_rows = keep.tile([P, UNITS], BF16)
         nc.vector.memset(bias_rows[:], 0.0)
-        plus_minus = keep.tile([P, P], BF16)
-        nc.vector.memset(plus_minus[:], 0.0)
-        nc.vector.memset(plus_minus[0:32, :], 1.0)
-        nc.vector.memset(plus_minus[32:64, :], -1.0)
+        pick = keep.tile([P, GATES - 1, P], BF16)
+        nc.vector.memset(pick[:], 0.0)
+        nc.vector.memset(pick[0:32, :, :], -1.0)
+        for j in range(1, GATES):
+            nc.vector.memset(pick[32 * j : 32 * (j + 1), j - 1, :], 1.0)
         halves = keep.tile([P, 2], F32)
         nc.vector.memset(halves[:, 0:1], -0.5)
         nc.vector.memset(halves[:, 1:2], 0.5)
@@ -93,27 +96,24 @@ def tile_multidimensinalgrucell_pb_kernel(
 
         states = keep.tile([P, GATES, ROW_TILES, UNITS], BF16)
         x_rows = keep.tile([P, ROW_TILES, UNITS], BF16)
-        nc.sync.dma_start(out=states[:, 1], in_=by_partition(left_state))
-        nc.sync.dma_start(out=states[:, 2], in_=by_partition(top_state))
-        nc.sync.dma_start(out=states[:, 3], in_=by_partition(diagonal_state))
-        nc.sync.dma_start(out=x_rows[:], in_=by_partition(x))
-        for j, bias in enumerate([b_zl, b_zt, b_zd]):
-            nc.sync.dma_start(out=bias_rows[0:1, j, :], in_=bias.unsqueeze(0))
-            nc.sync.dma_start(out=bias_rows[32:33, j, :], in_=b_zi.unsqueeze(0))
+        def load_rows(tile_rows, rows):
+            return lambda: nc.sync.dma_start(out=tile_rows, in_=by_partition(rows))
 
-        def load_scales(j):
-            for a in range(PASSES // PLANES_PER_TILE):
-                for quadrant in range(4):
-                    nc.sync.dma_start(
-                        out=w_planes[32 * quadrant : 32 * quadrant + 16, j, a, :].bitcast(I32),
-                        in_=gate_scales[j][
-                            PLANES_PER_TILE * a : PLANES_PER_TILE * (a + 1), 4 * quadrant : 4 * quadrant + 4, :
-                        ].bitcast(I32),
-                    )
+        def load_bias(j, bias):
+            return lambda: nc.sync.dma_start(out=bias_rows[32 * j : 32 * j + 1, :], in_=bias.unsqueeze(0))
 
-        def load_words(j, first_unit, width):
-            loads = []
-            for first_pass in range(0, PASSES, PASSES_PER_LOAD):
+        def load_scales(j, a, quadrant):
+            return lambda: nc.sync.dma_start(
+                out=w_planes[32 * quadrant : 32 * quadrant + 16, j, a, :].bitcast(I32),
+                in_=gate_scales[j][
+                    PLANES_PER_TILE * a : PLANES_PER_TILE * (a + 1), 4 * quadrant : 4 * quadrant + 4, :
+                ].bitcast(I32),
+            )
+
+        w_words = {}
+
+        def load_words(j, first_unit, width, first_pass):
+            def start():
                 words = weights.tile(
                     [P, PASSES_PER_LOAD, width],
                     I32,
@@ -127,20 +127,43 @@ def tile_multidimensinalgrucell_pb_kernel(
                     .rearrange("g p n t -> p g (n t)")[:, :, PACK * first_unit : PACK * (first_unit + width)]
                     .bitcast(I32),
                 )
-                loads.append(words)
-            return loads
+                w_words.setdefault((j, first_unit), []).append(words)
 
-        w_words = {}
-        for r in range(RANGES):
-            for j in (GATE_T, GATE_D, GATE_L):
-                if r == 0:
-                    load_scales(j)
-                w_words[(j, RANGE * r)] = load_words(j, RANGE * r, RANGE)
-                if r == 0 and j == GATE_T:
-                    nc.sync.dma_start(out=states[:, GATE_I], in_=by_partition(h_cand))
-        load_scales(GATE_I)
+            return start
+
+        def gate_loads(j, first_unit, width):
+            return [load_words(j, first_unit, width, first_pass) for first_pass in range(0, PASSES, PASSES_PER_LOAD)]
+
+        def scale_loads(j):
+            return [load_scales(j, a, quadrant) for a in range(PASSES // PLANES_PER_TILE) for quadrant in range(4)]
+
+        big = [
+            load_rows(states[:, 1], left_state),
+            load_rows(states[:, 2], top_state),
+            load_rows(states[:, 3], diagonal_state),
+            load_rows(x_rows[:], x),
+        ]
+        big.extend(gate_loads(GATE_T, 0, RANGE))
+        big.append(load_rows(states[:, GATE_I], h_cand))
+        big.extend(gate_loads(GATE_D, 0, RANGE))
+        big.extend(gate_loads(GATE_L, 0, RANGE))
+        for j in (GATE_T, GATE_D, GATE_L):
+            big.extend(gate_loads(j, RANGE, RANGE))
         for first_unit, width in LAST_PIECES:
-            w_words[(GATE_I, first_unit)] = load_words(GATE_I, first_unit, width)
+            big.extend(gate_loads(GATE_I, first_unit, width))
+        small = scale_loads(GATE_T)
+        small.extend([load_bias(j, bias) for j, bias in enumerate([b_zi, b_zl, b_zt, b_zd])])
+        for j in (GATE_D, GATE_L, GATE_I):
+            small.extend(scale_loads(j))
+        given = 0
+        with tc.manual_schedule(engines={mybir.EngineType.SP}):
+            for i, start_big in enumerate(big):
+                start_big()
+                count = SMALL_AFTER[i] if i < len(SMALL_AFTER) else 0
+                for start_small in small[given : given + count]:
+                    start_small()
+                given += count
+        assert given == len(small)
 
         q_codes = keep.tile([P, PASSES, BATCH], U32, align_bytes=64)
         q_planes = keep.tile([P, PASSES, BATCH], U8, align_bytes=64)
@@ -175,7 +198,7 @@ def tile_multidimensinalgrucell_pb_kernel(
             for half in range(UNITS // BANK):
                 half_cols = slice(BANK * half, BANK * (half + 1))
                 spread = psum.tile([P, BANK], F32, tag="bank")
-                nc.tensor.matmul(spread[:], lhsT=plus_minus[:], rhs=bias_rows[:, j, half_cols], start=True, stop=True)
+                nc.tensor.matmul(spread[:], lhsT=pick[:, j, :], rhs=bias_rows[:, half_cols], start=True, stop=True)
                 nc.scalar.copy(out=bias_less_i[:, j, half_cols], in_=spread[:])
 
         def multiply(j, first_unit, width):

@@ -33,8 +33,7 @@ PLANES_PER_TILE = 4
 PASSES_PER_LOAD = 4
 WEIGHT_BUFS = 11
 
-SMALL_AFTER = (2, 2, 2, 2, 4, 4, 4, 4, 4, 2, 2, 2, 2)
-SPLIT = True
+SMALL_AFTER = (2, 2, 2, 2, 4, 4, 4, 4, 4, 0, 0, 0, 0, 0, 0, 4, 4)
 
 FLOPS = 2 * BATCH * K * GATES * UNITS
 
@@ -165,6 +164,9 @@ def tile_multidimensinalgrucell_pb_kernel(
                 given += count
         assert given == len(small)
 
+        ctx.enter_context(
+            tc.manual_schedule(engines={mybir.EngineType.PE, mybir.EngineType.DVE, mybir.EngineType.Activation})
+        )
         q_codes = keep.tile([P, PASSES, BATCH], U32, align_bytes=64)
         q_planes = keep.tile([P, PASSES, BATCH], U8, align_bytes=64)
         q_parts = [states[:, 1], states[:, 2], states[:, 3], x_rows[:]]
@@ -193,107 +195,160 @@ def tile_multidimensinalgrucell_pb_kernel(
         nc.vector.tensor_tensor(out=gap_dl[:], in0=states[:, GATE_D], in1=states[:, GATE_L], op=ALU.subtract)
         nc.vector.tensor_tensor(out=gap_lh[:], in0=states[:, GATE_L], in1=states[:, GATE_I], op=ALU.subtract)
 
-        bias_less_i = keep.tile([P, GATES - 1, UNITS], F32)
-        for j in range(GATES - 1):
-            for half in range(UNITS // BANK):
-                half_cols = slice(BANK * half, BANK * (half + 1))
-                spread = psum.tile([P, BANK], F32, tag="bank")
-                nc.tensor.matmul(spread[:], lhsT=pick[:, j, :], rhs=bias_rows[:, half_cols], start=True, stop=True)
-                nc.scalar.copy(out=bias_less_i[:, j, half_cols], in_=spread[:])
+        TILES = range(ROW_TILES)
+
+        def cols_of(r):
+            return slice(RANGE * r, RANGE * (r + 1))
+
+        def vector(out, in0, in1, op):
+            nc.vector.tensor_tensor(out=out, in0=in0, in1=in1, op=op)
 
         def multiply(j, first_unit, width):
-            tiles_per_bank = BANK // width
-            banks = []
-            for first_tile in range(0, ROW_TILES, tiles_per_bank):
-                acc = psum.tile([P, tiles_per_bank, width], F32, tag="bank")
-                for i in range(tiles_per_bank):
-                    rows = slice(P * (first_tile + i), P * (first_tile + i + 1))
-                    for g in range(PASSES):
+            accs = []
+            for m in TILES:
+                acc = psum.tile([P, width], F32, name="acc_%d_%d_%d" % (j, first_unit, m), tag="bank")
+                accs.append(acc)
+            for load in range(PASSES // PASSES_PER_LOAD):
+                for m in TILES:
+                    rows = slice(P * m, P * (m + 1))
+                    for g in range(PASSES_PER_LOAD * load, PASSES_PER_LOAD * (load + 1)):
                         offset = 4 * (g % PLANES_PER_TILE)
                         nc.tensor.matmul_mx(
-                            out=acc[:, i, :],
+                            out=accs[m][:],
                             lhsT=q_codes[:, g, rows].bitcast(FP8X4),
                             lhsT_scale=q_planes[:, g, rows],
-                            rhs=w_words[(j, first_unit)][g // PASSES_PER_LOAD][:, g % PASSES_PER_LOAD, :].bitcast(FP8X4),
+                            rhs=w_words[(j, first_unit)][load][:, g % PASSES_PER_LOAD, :].bitcast(FP8X4),
                             rhs_scale=w_planes[offset:P, j, g // PLANES_PER_TILE, first_unit : first_unit + width],
                             start=(g == 0),
                             stop=(g == PASSES - 1),
                         )
-                banks.append((first_tile, tiles_per_bank, acc))
-            return banks
+            return accs
 
-        TILES = tuple(range(ROW_TILES)) if SPLIT else (slice(0, ROW_TILES),)
+        bias_less_i = keep.tile([P, GATES - 1, UNITS], F32)
 
-        def logits(j, r):
-            cols = slice(RANGE * r, RANGE * (r + 1))
+        def spread_biases():
+            for j in range(GATES - 1):
+                for half in range(UNITS // BANK):
+                    half_cols = slice(BANK * half, BANK * (half + 1))
+                    spread = psum.tile([P, BANK], F32, tag="bank")
+                    nc.tensor.matmul(spread[:], lhsT=pick[:, j, :], rhs=bias_rows[:, half_cols], start=True, stop=True)
+                    nc.scalar.copy(out=bias_less_i[:, j, half_cols], in_=spread[:])
+
+        def new_logit():
             logit = work.tile([P, ROW_TILES, RANGE], F32, name="logit", bufs=3)
-            for first_tile, tiles, acc in multiply(j, RANGE * r, RANGE):
-                nc.vector.tensor_tensor(
-                    out=logit[:, first_tile : first_tile + tiles],
-                    in0=acc[:],
-                    in1=bias_less_i[:, j - 1, cols].unsqueeze(1).to_broadcast([P, tiles, RANGE]),
-                    op=ALU.add,
-                )
             return logit
 
-        def join_logits(a, b, name):
-            share = work.tile([P, ROW_TILES, RANGE], F32, name="share")
-            larger = work.tile([P, ROW_TILES, RANGE], F32, name=name)
-            ln_larger = work.tile([P, ROW_TILES, RANGE], F32, name="ln_larger")
-            for m in TILES:
-                nc.vector.tensor_tensor(out=share[:, m], in0=a[:, m], in1=b[:, m], op=ALU.subtract)
-            for m in TILES:
-                nc.vector.tensor_tensor(out=larger[:, m], in0=a[:, m], in1=b[:, m], op=ALU.max)
-            for m in TILES:
-                nc.scalar.activation(out=share[:, m], in_=share[:, m], func=ACT.Sigmoid)
+        def add_bias(logit, j, r, accs, m):
+            vector(logit[:, m], accs[m][:], bias_less_i[:, j - 1, cols_of(r)], ALU.add)
+
+        def sigmoid(share, part):
+            nc.scalar.activation(out=share[:, part], in_=share[:, part], func=ACT.Sigmoid)
+
+        def ln_of_larger_share(ln_larger, share):
             for m in TILES:
                 nc.scalar.activation(out=ln_larger[:, m], in_=share[:, m], func=ACT.Abs, bias=halves[:, 0:1])
             for m in TILES:
                 nc.scalar.activation(out=ln_larger[:, m], in_=ln_larger[:, m], func=ACT.Ln, bias=halves[:, 1:2])
-            return share, larger, ln_larger
 
-        def both(out, in0, in1, op):
+        def first_join(r, logit_t):
+            accs = multiply(GATE_D, RANGE * r, RANGE)
+            logit_d = new_logit()
+            share = work.tile([P, ROW_TILES, RANGE], F32, name="share")
+            larger = work.tile([P, ROW_TILES, RANGE], F32, name="lse_of_two")
+            ln_larger = work.tile([P, ROW_TILES, RANGE], F32, name="ln_larger")
+            blend = work.tile([P, ROW_TILES, RANGE], F32, name="blend")
             for m in TILES:
-                nc.vector.tensor_tensor(out=out[:, m], in0=in0[:, m], in1=in1[:, m], op=op)
+                add_bias(logit_d, GATE_D, r, accs, m)
+                vector(share[:, m], logit_t[:, m], logit_d[:, m], ALU.subtract)
+            for m in TILES:
+                vector(larger[:, m], logit_t[:, m], logit_d[:, m], ALU.max)
+            for m in TILES:
+                sigmoid(share, m)
+            ln_of_larger_share(ln_larger, share)
+            for m in TILES:
+                vector(blend[:, m], share[:, m], gap_td[:, m, cols_of(r)], ALU.mult)
+            for m in TILES:
+                vector(blend[:, m], blend[:, m], gap_dl[:, m, cols_of(r)], ALU.add)
+            return larger, ln_larger, blend
+
+        def logits_of(j, r):
+            accs = multiply(j, RANGE * r, RANGE)
+            logit = new_logit()
+            for m in TILES:
+                add_bias(logit, j, r, accs, m)
+            return logit
+
+        def finish_lse(larger, ln_larger):
+            for m in TILES:
+                vector(larger[:, m], larger[:, m], ln_larger[:, m], ALU.subtract)
+
+        def last_differences(lse, first_unit, width):
+            r = first_unit // RANGE
+            inside = slice(first_unit - RANGE * r, first_unit - RANGE * r + width)
+            accs = multiply(GATE_I, first_unit, width)
+            share = work.tile([P, ROW_TILES, width], F32, name="share")
+            for m in TILES:
+                vector(share[:, m], lse[:, m, inside], accs[m][:], ALU.subtract)
+            return share
+
+        def last_blend(blend, share, first_unit, width, parts):
+            r = first_unit // RANGE
+            inside = slice(first_unit - RANGE * r, first_unit - RANGE * r + width)
+            for part in parts:
+                vector(blend[:, part, inside], blend[:, part, inside], share[:, part], ALU.mult)
+            for part in parts:
+                vector(
+                    blend[:, part, inside],
+                    blend[:, part, inside],
+                    states[:, GATE_I, part, first_unit : first_unit + width],
+                    ALU.add,
+                )
+            nc.sync.dma_start(out=by_partition(out)[:, :, first_unit : first_unit + width], in_=blend[:, :, inside])
+
+        BOTH = (slice(0, ROW_TILES),)
+
+        accs_t = multiply(GATE_T, 0, RANGE)
+        spread_biases()
+        logit_t = new_logit()
+        for m in TILES:
+            add_bias(logit_t, GATE_T, 0, accs_t, m)
 
         lse_of_three = []
         blends = []
         for r in range(RANGES):
-            cols = slice(RANGE * r, RANGE * (r + 1))
-            logit_t = logits(GATE_T, r)
-            logit_d = logits(GATE_D, r)
-            share, lse, ln_larger = join_logits(logit_t, logit_d, "lse_of_two")
-            blend = work.tile([P, ROW_TILES, RANGE], F32, name="blend")
-            both(blend, share, gap_td[:, :, cols], ALU.mult)
-            both(blend, blend, gap_dl[:, :, cols], ALU.add)
-            logit_l = logits(GATE_L, r)
-            both(lse, lse, ln_larger, ALU.subtract)
-            share, lse, ln_larger = join_logits(lse, logit_l, "lse_of_three")
-            both(blend, blend, share, ALU.mult)
-            both(blend, blend, gap_lh[:, :, cols], ALU.add)
-            both(lse, lse, ln_larger, ALU.subtract)
-            lse_of_three.append(lse)
+            larger, ln_larger, blend = first_join(r, logit_t)
             blends.append(blend)
+            logit_l = logits_of(GATE_L, r)
+            finish_lse(larger, ln_larger)
+            share = work.tile([P, ROW_TILES, RANGE], F32, name="share")
+            larger_2 = work.tile([P, ROW_TILES, RANGE], F32, name="lse_of_three")
+            ln_larger_2 = work.tile([P, ROW_TILES, RANGE], F32, name="ln_larger")
+            for m in TILES:
+                vector(share[:, m], larger[:, m], logit_l[:, m], ALU.subtract)
+            if r == RANGES - 1:
+                first_unit, width = LAST_PIECES[0]
+                share_0 = last_differences(lse_of_three[0], first_unit, width)
+            for m in TILES:
+                vector(larger_2[:, m], larger[:, m], logit_l[:, m], ALU.max)
+            for m in TILES:
+                sigmoid(share, m)
+            if r == RANGES - 1:
+                for m in TILES:
+                    sigmoid(share_0, m)
+            ln_of_larger_share(ln_larger_2, share)
+            for m in TILES:
+                vector(blend[:, m], blend[:, m], share[:, m], ALU.mult)
+            for m in TILES:
+                vector(blend[:, m], blend[:, m], gap_lh[:, m, cols_of(r)], ALU.add)
+            if r < RANGES - 1:
+                logit_t = logits_of(GATE_T, r + 1)
+            else:
+                last_blend(blends[0], share_0, first_unit, width, TILES)
+            finish_lse(larger_2, ln_larger_2)
+            lse_of_three.append(larger_2)
 
-        for first_unit, width in LAST_PIECES:
-            r = first_unit // RANGE
-            inside = slice(first_unit - RANGE * r, first_unit - RANGE * r + width)
-            share = work.tile([P, ROW_TILES, width], F32, name="share")
-            parts = []
-            for first_tile, tiles, acc in multiply(GATE_I, first_unit, width):
-                part = slice(first_tile, first_tile + tiles)
-                parts.append(part)
-                nc.vector.tensor_tensor(out=share[:, part], in0=lse_of_three[r][:, part, inside], in1=acc[:], op=ALU.subtract)
-            for part in parts:
-                nc.scalar.activation(out=share[:, part], in_=share[:, part], func=ACT.Sigmoid)
-            result = blends[r]
-            for part in parts:
-                nc.vector.tensor_tensor(out=result[:, part, inside], in0=result[:, part, inside], in1=share[:, part], op=ALU.mult)
-            for part in parts:
-                nc.vector.tensor_tensor(
-                    out=result[:, part, inside],
-                    in0=result[:, part, inside],
-                    in1=states[:, GATE_I, part, first_unit : first_unit + width],
-                    op=ALU.add,
-                )
-            nc.scalar.dma_start(out=by_partition(out)[:, :, first_unit : first_unit + width], in_=result[:, :, inside])
+        shares = [last_differences(lse_of_three[1], first_unit, width) for first_unit, width in LAST_PIECES[1:]]
+        for share in shares:
+            sigmoid(share, BOTH[0])
+        for share, (first_unit, width) in zip(shares, LAST_PIECES[1:]):
+            last_blend(blends[1], share, first_unit, width, BOTH)

@@ -33,7 +33,7 @@ PLANES_PER_TILE = 4
 PASSES_PER_LOAD = 4
 WEIGHT_BUFS = 11
 
-SMALL_AFTER = (2, 2, 2, 2, 4, 4, 4, 4, 4, 0, 0, 0, 0, 0, 0, 4, 4)
+SMALL_AFTER = (2, 2, 2, 2, 2, 2, 2, 2)
 
 FLOPS = 2 * BATCH * K * GATES * UNITS
 
@@ -99,14 +99,14 @@ def tile_multidimensinalgrucell_pb_kernel(
             return lambda: nc.sync.dma_start(out=tile_rows, in_=by_partition(rows))
 
         def load_bias(j, bias):
-            return lambda: nc.sync.dma_start(out=bias_rows[32 * j : 32 * j + 1, :], in_=bias.unsqueeze(0))
+            return lambda: nc.gpsimd.dma_start(out=bias_rows[32 * j : 32 * j + 1, :], in_=bias.unsqueeze(0))
 
-        def load_scales(j, a, quadrant):
-            return lambda: nc.sync.dma_start(
-                out=w_planes[32 * quadrant : 32 * quadrant + 16, j, a, :].bitcast(I32),
+        def load_scales(j, a, quadrant, queue, word):
+            return lambda: queue.dma_start(
+                out=w_planes[32 * quadrant : 32 * quadrant + 16, j, a, :].bitcast(word),
                 in_=gate_scales[j][
                     PLANES_PER_TILE * a : PLANES_PER_TILE * (a + 1), 4 * quadrant : 4 * quadrant + 4, :
-                ].bitcast(I32),
+                ].bitcast(word),
             )
 
         w_words = {}
@@ -133,8 +133,10 @@ def tile_multidimensinalgrucell_pb_kernel(
         def gate_loads(j, first_unit, width):
             return [load_words(j, first_unit, width, first_pass) for first_pass in range(0, PASSES, PASSES_PER_LOAD)]
 
-        def scale_loads(j):
-            return [load_scales(j, a, quadrant) for a in range(PASSES // PLANES_PER_TILE) for quadrant in range(4)]
+        def scale_loads(j, queue, word):
+            return [
+                load_scales(j, a, quadrant, queue, word) for a in range(PASSES // PLANES_PER_TILE) for quadrant in range(4)
+            ]
 
         big = [
             load_rows(states[:, 1], left_state),
@@ -150,10 +152,13 @@ def tile_multidimensinalgrucell_pb_kernel(
             big.extend(gate_loads(j, RANGE, RANGE))
         for first_unit, width in LAST_PIECES:
             big.extend(gate_loads(GATE_I, first_unit, width))
-        small = scale_loads(GATE_T)
-        small.extend([load_bias(j, bias) for j, bias in enumerate([b_zi, b_zl, b_zt, b_zd])])
-        for j in (GATE_D, GATE_L, GATE_I):
-            small.extend(scale_loads(j))
+        small = scale_loads(GATE_T, nc.sync, I32)
+        small.extend(scale_loads(GATE_D, nc.sync, I32))
+        aside = [load_bias(j, bias) for j, bias in enumerate([b_zi, b_zl, b_zt, b_zd])]
+        for j in (GATE_L, GATE_I):
+            aside.extend(scale_loads(j, nc.gpsimd, F32))
+        for start_aside in aside:
+            start_aside()
         given = 0
         with tc.manual_schedule(engines={mybir.EngineType.SP}):
             for i, start_big in enumerate(big):

@@ -272,8 +272,6 @@ def tile_multidimensinalgrucell_pb_kernel(
             ln_of_larger_share(ln_larger, share)
             for m in TILES:
                 vector(blend[:, m], share[:, m], gap_td[:, m, cols_of(r)], ALU.mult)
-            for m in TILES:
-                vector(blend[:, m], blend[:, m], gap_dl[:, m, cols_of(r)], ALU.add)
             return larger, ln_larger, blend
 
         def logits_of(j, r):
@@ -323,7 +321,9 @@ def tile_multidimensinalgrucell_pb_kernel(
         for r in range(RANGES):
             larger, ln_larger, blend = first_join(r, logit_t)
             blends.append(blend)
+            nc.gpsimd.tensor_tensor(out=blend[:, 0], in0=blend[:, 0], in1=gap_dl[:, 0, cols_of(r)], op=ALU.add)
             logit_l = logits_of(GATE_L, r)
+            vector(blend[:, 1], blend[:, 1], gap_dl[:, 1, cols_of(r)], ALU.add)
             finish_lse(larger, ln_larger)
             share = work.tile([P, ROW_TILES, RANGE], F32, name="share")
             larger_2 = work.tile([P, ROW_TILES, RANGE], F32, name="lse_of_three")
@@ -343,11 +343,13 @@ def tile_multidimensinalgrucell_pb_kernel(
             ln_of_larger_share(ln_larger_2, share)
             for m in TILES:
                 vector(blend[:, m], blend[:, m], share[:, m], ALU.mult)
-            for m in TILES:
-                vector(blend[:, m], blend[:, m], gap_lh[:, m, cols_of(r)], ALU.add)
             if r < RANGES - 1:
+                nc.gpsimd.tensor_tensor(out=blend[:, 0], in0=blend[:, 0], in1=gap_lh[:, 0, cols_of(r)], op=ALU.add)
                 logit_t = logits_of(GATE_T, r + 1)
+                vector(blend[:, 1], blend[:, 1], gap_lh[:, 1, cols_of(r)], ALU.add)
             else:
+                for m in TILES:
+                    vector(blend[:, m], blend[:, m], gap_lh[:, m, cols_of(r)], ALU.add)
                 last_blend(blends[0], share_0, first_unit, width, TILES)
             finish_lse(larger_2, ln_larger_2)
             lse_of_three.append(larger_2)

@@ -33,6 +33,7 @@ PLANES_PER_TILE = 4
 PASSES_PER_LOAD = 4
 WEIGHT_BUFS = 11
 
+GPSIMD_ADDS = True
 SMALL_AFTER = (2, 2, 2, 2, 2, 2, 2, 2)
 
 FLOPS = 2 * BATCH * K * GATES * UNITS
@@ -249,30 +250,79 @@ def tile_multidimensinalgrucell_pb_kernel(
         def sigmoid(share, part):
             nc.scalar.activation(out=share[:, part], in_=share[:, part], func=ACT.Sigmoid)
 
-        def ln_of_larger_share(ln_larger, share):
+        tiles_of = [{}, {}]
+
+        def gate_t(r):
+            tiles_of[r]["logit_t"] = logits_of(GATE_T, r)
+
+        def first_differences(r):
+            t = tiles_of[r]
+            accs = multiply(GATE_D, RANGE * r, RANGE)
+            t["logit_d"] = new_logit()
+            share = work.tile([P, ROW_TILES, RANGE], F32, name="share")
+            t["share"] = share
             for m in TILES:
-                nc.scalar.activation(out=ln_larger[:, m], in_=share[:, m], func=ACT.Abs, bias=halves[:, 0:1])
+                add_bias(t["logit_d"], GATE_D, r, accs, m)
+                vector(share[:, m], t["logit_t"][:, m], t["logit_d"][:, m], ALU.subtract)
+
+        def first_maxima(r):
+            t = tiles_of[r]
+            larger = work.tile([P, ROW_TILES, RANGE], F32, name="lse_of_two")
+            t["lse"] = larger
+            for m in TILES:
+                vector(larger[:, m], t["logit_t"][:, m], t["logit_d"][:, m], ALU.max)
+
+        def shares(r):
+            t = tiles_of[r]
+            ln_larger = work.tile([P, ROW_TILES, RANGE], F32, name="ln_larger")
+            t["ln"] = ln_larger
+            for m in TILES:
+                sigmoid(t["share"], m)
+            for m in TILES:
+                nc.scalar.activation(out=ln_larger[:, m], in_=t["share"][:, m], func=ACT.Abs, bias=halves[:, 0:1])
+
+        def logarithms(r):
+            ln_larger = tiles_of[r]["ln"]
             for m in TILES:
                 nc.scalar.activation(out=ln_larger[:, m], in_=ln_larger[:, m], func=ACT.Ln, bias=halves[:, 1:2])
 
-        def first_join(r, logit_t):
-            accs = multiply(GATE_D, RANGE * r, RANGE)
-            logit_d = new_logit()
-            share = work.tile([P, ROW_TILES, RANGE], F32, name="share")
-            larger = work.tile([P, ROW_TILES, RANGE], F32, name="lse_of_two")
-            ln_larger = work.tile([P, ROW_TILES, RANGE], F32, name="ln_larger")
+        def first_products(r):
+            t = tiles_of[r]
             blend = work.tile([P, ROW_TILES, RANGE], F32, name="blend")
+            t["blend"] = blend
             for m in TILES:
-                add_bias(logit_d, GATE_D, r, accs, m)
-                vector(share[:, m], logit_t[:, m], logit_d[:, m], ALU.subtract)
+                vector(blend[:, m], t["share"][:, m], gap_td[:, m, cols_of(r)], ALU.mult)
+
+        def products(r):
+            t = tiles_of[r]
             for m in TILES:
-                vector(larger[:, m], logit_t[:, m], logit_d[:, m], ALU.max)
+                vector(t["blend"][:, m], t["blend"][:, m], t["share"][:, m], ALU.mult)
+
+        def add_gap(r, gap, m, engine):
+            blend = tiles_of[r]["blend"]
+            engine.tensor_tensor(out=blend[:, m], in0=blend[:, m], in1=gap[:, m, cols_of(r)], op=ALU.add)
+
+        def gate_l(r):
+            tiles_of[r]["logit_l"] = logits_of(GATE_L, r)
+
+        def finish_lse(r):
+            t = tiles_of[r]
             for m in TILES:
-                sigmoid(share, m)
-            ln_of_larger_share(ln_larger, share)
+                vector(t["lse"][:, m], t["lse"][:, m], t["ln"][:, m], ALU.subtract)
+
+        def second_differences(r):
+            t = tiles_of[r]
+            share = work.tile([P, ROW_TILES, RANGE], F32, name="share")
+            t["share"] = share
             for m in TILES:
-                vector(blend[:, m], share[:, m], gap_td[:, m, cols_of(r)], ALU.mult)
-            return larger, ln_larger, blend
+                vector(share[:, m], t["lse"][:, m], t["logit_l"][:, m], ALU.subtract)
+
+        def second_maxima(r):
+            t = tiles_of[r]
+            larger = work.tile([P, ROW_TILES, RANGE], F32, name="lse_of_three")
+            for m in TILES:
+                vector(larger[:, m], t["lse"][:, m], t["logit_l"][:, m], ALU.max)
+            t["lse"] = larger
 
         def logits_of(j, r):
             accs = multiply(j, RANGE * r, RANGE)
@@ -281,21 +331,18 @@ def tile_multidimensinalgrucell_pb_kernel(
                 add_bias(logit, j, r, accs, m)
             return logit
 
-        def finish_lse(larger, ln_larger):
-            for m in TILES:
-                vector(larger[:, m], larger[:, m], ln_larger[:, m], ALU.subtract)
-
-        def last_differences(lse, first_unit, width):
+        def last_differences(first_unit, width):
             r = first_unit // RANGE
             inside = slice(first_unit - RANGE * r, first_unit - RANGE * r + width)
             accs = multiply(GATE_I, first_unit, width)
             share = work.tile([P, ROW_TILES, width], F32, name="share")
             for m in TILES:
-                vector(share[:, m], lse[:, m, inside], accs[m][:], ALU.subtract)
+                vector(share[:, m], tiles_of[r]["lse"][:, m, inside], accs[m][:], ALU.subtract)
             return share
 
-        def last_blend(blend, share, first_unit, width, parts):
+        def last_blend(share, first_unit, width, parts):
             r = first_unit // RANGE
+            blend = tiles_of[r]["blend"]
             inside = slice(first_unit - RANGE * r, first_unit - RANGE * r + width)
             for part in parts:
                 vector(blend[:, part, inside], blend[:, part, inside], share[:, part], ALU.mult)
@@ -309,53 +356,55 @@ def tile_multidimensinalgrucell_pb_kernel(
             nc.sync.dma_start(out=by_partition(out)[:, :, first_unit : first_unit + width], in_=blend[:, :, inside])
 
         BOTH = (slice(0, ROW_TILES),)
+        HELPER = nc.gpsimd if GPSIMD_ADDS else nc.vector
 
         accs_t = multiply(GATE_T, 0, RANGE)
         spread_biases()
-        logit_t = new_logit()
+        tiles_of[0]["logit_t"] = new_logit()
         for m in TILES:
-            add_bias(logit_t, GATE_T, 0, accs_t, m)
-
-        lse_of_three = []
-        blends = []
-        for r in range(RANGES):
-            larger, ln_larger, blend = first_join(r, logit_t)
-            blends.append(blend)
-            nc.gpsimd.tensor_tensor(out=blend[:, 0], in0=blend[:, 0], in1=gap_dl[:, 0, cols_of(r)], op=ALU.add)
-            logit_l = logits_of(GATE_L, r)
-            vector(blend[:, 1], blend[:, 1], gap_dl[:, 1, cols_of(r)], ALU.add)
-            finish_lse(larger, ln_larger)
-            share = work.tile([P, ROW_TILES, RANGE], F32, name="share")
-            larger_2 = work.tile([P, ROW_TILES, RANGE], F32, name="lse_of_three")
-            ln_larger_2 = work.tile([P, ROW_TILES, RANGE], F32, name="ln_larger")
-            for m in TILES:
-                vector(share[:, m], larger[:, m], logit_l[:, m], ALU.subtract)
-            if r == RANGES - 1:
-                first_unit, width = LAST_PIECES[0]
-                share_0 = last_differences(lse_of_three[0], first_unit, width)
-            for m in TILES:
-                vector(larger_2[:, m], larger[:, m], logit_l[:, m], ALU.max)
-            for m in TILES:
-                sigmoid(share, m)
-            if r == RANGES - 1:
-                for m in TILES:
-                    sigmoid(share_0, m)
-            ln_of_larger_share(ln_larger_2, share)
-            for m in TILES:
-                vector(blend[:, m], blend[:, m], share[:, m], ALU.mult)
-            if r < RANGES - 1:
-                nc.gpsimd.tensor_tensor(out=blend[:, 0], in0=blend[:, 0], in1=gap_lh[:, 0, cols_of(r)], op=ALU.add)
-                logit_t = logits_of(GATE_T, r + 1)
-                vector(blend[:, 1], blend[:, 1], gap_lh[:, 1, cols_of(r)], ALU.add)
-            else:
-                for m in TILES:
-                    vector(blend[:, m], blend[:, m], gap_lh[:, m, cols_of(r)], ALU.add)
-                last_blend(blends[0], share_0, first_unit, width, TILES)
-            finish_lse(larger_2, ln_larger_2)
-            lse_of_three.append(larger_2)
-
-        shares = [last_differences(lse_of_three[1], first_unit, width) for first_unit, width in LAST_PIECES[1:]]
-        for share in shares:
+            add_bias(tiles_of[0]["logit_t"], GATE_T, 0, accs_t, m)
+        first_differences(0)
+        first_maxima(0)
+        shares(0)
+        logarithms(0)
+        first_products(0)
+        add_gap(0, gap_dl, 0, HELPER)
+        gate_l(0)
+        add_gap(0, gap_dl, 1, nc.vector)
+        finish_lse(0)
+        second_differences(0)
+        second_maxima(0)
+        shares(0)
+        gate_t(1)
+        products(0)
+        add_gap(0, gap_lh, 0, HELPER)
+        first_differences(1)
+        add_gap(0, gap_lh, 1, nc.vector)
+        first_maxima(1)
+        shares(1)
+        logarithms(1)
+        logarithms(0)
+        first_products(1)
+        add_gap(1, gap_dl, 0, HELPER)
+        gate_l(1)
+        add_gap(1, gap_dl, 1, nc.vector)
+        finish_lse(1)
+        second_differences(1)
+        finish_lse(0)
+        first_unit, width = LAST_PIECES[0]
+        share_0 = last_differences(first_unit, width)
+        second_maxima(1)
+        shares(1)
+        for m in TILES:
+            sigmoid(share_0, m)
+        logarithms(1)
+        products(1)
+        for m in TILES:
+            add_gap(1, gap_lh, m, nc.vector)
+        last_blend(share_0, first_unit, width, TILES)
+        finish_lse(1)
+        last_shares = [last_differences(first_unit, width) for first_unit, width in LAST_PIECES[1:]]
+        for share in last_shares:
             sigmoid(share, BOTH[0])
-        for share, (first_unit, width) in zip(shares, LAST_PIECES[1:]):
-            last_blend(blends[1], share, first_unit, width, BOTH)
+        for share, (first_unit, width) in zip(last_shares, LAST_PIECES[1:]):
+            last_blend(share, first_unit, width, BOTH)

from contextlib import ExitStack

import concourse.mybir as mybir
from concourse.masks import make_identity

F32 = mybir.dt.float32
BF16 = mybir.dt.bfloat16
I32 = mybir.dt.int32
U32 = mybir.dt.uint32
U8 = mybir.dt.uint8
FP8X4 = mybir.dt.float8_e4m3fn_x4
ALU = mybir.AluOpType
ACT = mybir.ActivationFunctionType

P = 128
PACK = 4
K_PASS = P * PACK
BATCH = 256
UNITS = 1024
K = 4 * UNITS
PASSES = K // K_PASS
ROW_TILES = BATCH // P
GATES = 4
GATE_I = 0
GATE_L = 1
GATE_T = 2
GATE_D = 3
BANK = 512
RANGE = BANK
RANGES = UNITS // RANGE
LAST_PIECES = ((0, RANGE), (RANGE, RANGE // 2), (RANGE + RANGE // 2, RANGE // 2))
PLANES_PER_TILE = 4
PASSES_PER_LOAD = 4
WEIGHT_BUFS = 11

GPSIMD_ADDS = True
SMALL_AFTER = (2, 2, 2, 2, 2, 2, 2, 2)

FLOPS = 2 * BATCH * K * GATES * UNITS


def tile_multidimensinalgrucell_pb_kernel(
    tc,
    x,
    left_state,
    top_state,
    diagonal_state,
    h_cand,
    w_zi_words,
    w_zi_scales,
    b_zi,
    w_zl_words,
    w_zl_scales,
    b_zl,
    w_zt_words,
    w_zt_scales,
    b_zt,
    w_zd_words,
    w_zd_scales,
    b_zd,
    out,
):
    nc = tc.nc
    gate_words = [w_zi_words, w_zl_words, w_zt_words, w_zd_words]
    gate_scales = [w_zi_scales, w_zl_scales, w_zt_scales, w_zd_scales]

    with ExitStack() as ctx:
        keep = ctx.enter_context(tc.tile_pool(name="keep", bufs=1))
        stage = ctx.enter_context(tc.tile_pool(name="stage", bufs=4))
        weights = ctx.enter_context(tc.tile_pool(name="weights", bufs=WEIGHT_BUFS))
        work = ctx.enter_context(tc.tile_pool(name="work", bufs=2))
        psum = ctx.enter_context(tc.psum_pool(name="psum", bufs=8))

        identity = keep.tile([P, P], F32)
        make_identity(nc, identity[:])

        w_planes = keep.tile([P, GATES, PASSES // PLANES_PER_TILE, UNITS], U8, align_bytes=64)
        for j in (GATE_T, GATE_D, GATE_L, GATE_I):
            nc.vector.memset(w_planes[:, j].rearrange("p a n -> p (a n)").bitcast(I32), 0)

        bias_rows = keep.tile([P, UNITS], BF16)
        nc.vector.memset(bias_rows[:], 0.0)
        pick = keep.tile([P, GATES - 1, P], BF16)
        nc.vector.memset(pick[:], 0.0)
        nc.vector.memset(pick[0:32, :, :], -1.0)
        for j in range(1, GATES):
            nc.vector.memset(pick[32 * j : 32 * (j + 1), j - 1, :], 1.0)
        halves = keep.tile([P, 2], F32)
        nc.vector.memset(halves[:, 0:1], -0.5)
        nc.vector.memset(halves[:, 1:2], 0.5)
        warm = keep.tile([P, 1], F32)
        nc.scalar.activation(out=warm[:], in_=halves[:, 0:1], func=ACT.Sigmoid)

        def by_partition(rows):
            return rows.rearrange("(p m) u -> p m u", m=ROW_TILES)

        states = keep.tile([P, GATES, ROW_TILES, UNITS], BF16)
        x_rows = keep.tile([P, ROW_TILES, UNITS], BF16)
        def load_rows(tile_rows, rows):
            return lambda: nc.sync.dma_start(out=tile_rows, in_=by_partition(rows))

        def load_bias(j, bias):
            return lambda: nc.gpsimd.dma_start(out=bias_rows[32 * j : 32 * j + 1, :], in_=bias.unsqueeze(0))

        def load_scales(j, a, quadrant, queue, word):
            return lambda: queue.dma_start(
                out=w_planes[32 * quadrant : 32 * quadrant + 16, j, a, :].bitcast(word),
                in_=gate_scales[j][
                    PLANES_PER_TILE * a : PLANES_PER_TILE * (a + 1), 4 * quadrant : 4 * quadrant + 4, :
                ].bitcast(word),
            )

        w_words = {}

        def load_words(j, first_unit, width, first_pass):
            def start():
                words = weights.tile(
                    [P, PASSES_PER_LOAD, width],
                    I32,
                    name="words_%d_%d_%d" % (j, first_unit, first_pass),
                    tag="words",
                    align_bytes=64,
                )
                nc.sync.dma_start(
                    out=words[:],
                    in_=gate_words[j][first_pass : first_pass + PASSES_PER_LOAD]
                    .rearrange("g p n t -> p g (n t)")[:, :, PACK * first_unit : PACK * (first_unit + width)]
                    .bitcast(I32),
                )
                w_words.setdefault((j, first_unit), []).append(words)

            return start

        def gate_loads(j, first_unit, width):
            return [load_words(j, first_unit, width, first_pass) for first_pass in range(0, PASSES, PASSES_PER_LOAD)]

        def scale_loads(j, queue, word):
            return [
                load_scales(j, a, quadrant, queue, word) for a in range(PASSES // PLANES_PER_TILE) for quadrant in range(4)
            ]

        big = [
            load_rows(states[:, 1], left_state),
            load_rows(states[:, 2], top_state),
            load_rows(states[:, 3], diagonal_state),
            load_rows(x_rows[:], x),
        ]
        big.extend(gate_loads(GATE_T, 0, RANGE))
        big.append(load_rows(states[:, GATE_I], h_cand))
        big.extend(gate_loads(GATE_D, 0, RANGE))
        big.extend(gate_loads(GATE_L, 0, RANGE))
        for j in (GATE_T, GATE_D, GATE_L):
            big.extend(gate_loads(j, RANGE, RANGE))
        for first_unit, width in LAST_PIECES:
            big.extend(gate_loads(GATE_I, first_unit, width))
        small = scale_loads(GATE_T, nc.sync, I32)
        small.extend(scale_loads(GATE_D, nc.sync, I32))
        aside = [load_bias(j, bias) for j, bias in enumerate([b_zi, b_zl, b_zt, b_zd])]
        for j in (GATE_L, GATE_I):
            aside.extend(scale_loads(j, nc.gpsimd, F32))
        for start_aside in aside:
            start_aside()
        given = 0
        with tc.manual_schedule(engines={mybir.EngineType.SP}):
            for i, start_big in enumerate(big):
                start_big()
                count = SMALL_AFTER[i] if i < len(SMALL_AFTER) else 0
                for start_small in small[given : given + count]:
                    start_small()
                given += count
        assert given == len(small)

        ctx.enter_context(
            tc.manual_schedule(engines={mybir.EngineType.PE, mybir.EngineType.DVE, mybir.EngineType.Activation})
        )
        q_codes = keep.tile([P, PASSES, BATCH], U32, align_bytes=64)
        q_planes = keep.tile([P, PASSES, BATCH], U8, align_bytes=64)
        q_parts = [states[:, 1], states[:, 2], states[:, 3], x_rows[:]]
        for g in range(PASSES):
            part = q_parts[g // 2]
            first_word = (g % 2) * (K_PASS // 2)
            flipped = psum.tile([P, 2, BATCH], F32, tag="bank")
            for u in range(2):
                for m in range(ROW_TILES):
                    nc.tensor.transpose(
                        flipped[:, u, P * m : P * (m + 1)],
                        part[:, m, :].bitcast(F32)[:, first_word + u : first_word + K_PASS // 2 : 2],
                        identity[:],
                    )
            grouped = stage.tile([P, PACK * BATCH], BF16, align_bytes=64)
            nc.scalar.copy(
                out=grouped[:].bitcast(F32).rearrange("p (r u) -> p r u", u=2),
                in_=flipped[:].rearrange("p u r -> p r u"),
            )
            nc.vector.quantize_mx(out=q_codes[:, g, :].bitcast(FP8X4), scales=q_planes[:, g, :], in_=grouped[:])

        gap_td = keep.tile([P, ROW_TILES, UNITS], F32)
        gap_dl = keep.tile([P, ROW_TILES, UNITS], F32)
        gap_lh = keep.tile([P, ROW_TILES, UNITS], F32)
        nc.vector.tensor_tensor(out=gap_td[:], in0=states[:, GATE_T], in1=states[:, GATE_D], op=ALU.subtract)
        nc.vector.tensor_tensor(out=gap_dl[:], in0=states[:, GATE_D], in1=states[:, GATE_L], op=ALU.subtract)
        nc.vector.tensor_tensor(out=gap_lh[:], in0=states[:, GATE_L], in1=states[:, GATE_I], op=ALU.subtract)

        TILES = range(ROW_TILES)

        def cols_of(r):
            return slice(RANGE * r, RANGE * (r + 1))

        def vector(out, in0, in1, op):
            nc.vector.tensor_tensor(out=out, in0=in0, in1=in1, op=op)

        def multiply(j, first_unit, width):
            accs = []
            for m in TILES:
                acc = psum.tile([P, width], F32, name="acc_%d_%d_%d" % (j, first_unit, m), tag="bank")
                accs.append(acc)
            for load in range(PASSES // PASSES_PER_LOAD):
                for m in TILES:
                    rows = slice(P * m, P * (m + 1))
                    for g in range(PASSES_PER_LOAD * load, PASSES_PER_LOAD * (load + 1)):
                        offset = 4 * (g % PLANES_PER_TILE)
                        nc.tensor.matmul_mx(
                            out=accs[m][:],
                            lhsT=q_codes[:, g, rows].bitcast(FP8X4),
                            lhsT_scale=q_planes[:, g, rows],
                            rhs=w_words[(j, first_unit)][load][:, g % PASSES_PER_LOAD, :].bitcast(FP8X4),
                            rhs_scale=w_planes[offset:P, j, g // PLANES_PER_TILE, first_unit : first_unit + width],
                            start=(g == 0),
                            stop=(g == PASSES - 1),
                        )
            return accs

        bias_less_i = keep.tile([P, GATES - 1, UNITS], F32)

        def spread_biases():
            for j in range(GATES - 1):
                for half in range(UNITS // BANK):
                    half_cols = slice(BANK * half, BANK * (half + 1))
                    spread = psum.tile([P, BANK], F32, tag="bank")
                    nc.tensor.matmul(spread[:], lhsT=pick[:, j, :], rhs=bias_rows[:, half_cols], start=True, stop=True)
                    nc.scalar.copy(out=bias_less_i[:, j, half_cols], in_=spread[:])

        def new_logit():
            logit = work.tile([P, ROW_TILES, RANGE], F32, name="logit", bufs=3)
            return logit

        def add_bias(logit, j, r, accs, m):
            vector(logit[:, m], accs[m][:], bias_less_i[:, j - 1, cols_of(r)], ALU.add)

        def sigmoid(share, part):
            nc.scalar.activation(out=share[:, part], in_=share[:, part], func=ACT.Sigmoid)

        tiles_of = [{}, {}]

        def gate_t(r):
            tiles_of[r]["logit_t"] = logits_of(GATE_T, r)

        def first_differences(r):
            t = tiles_of[r]
            accs = multiply(GATE_D, RANGE * r, RANGE)
            t["logit_d"] = new_logit()
            share = work.tile([P, ROW_TILES, RANGE], F32, name="share")
            t["share"] = share
            for m in TILES:
                add_bias(t["logit_d"], GATE_D, r, accs, m)
                vector(share[:, m], t["logit_t"][:, m], t["logit_d"][:, m], ALU.subtract)

        def first_maxima(r):
            t = tiles_of[r]
            larger = work.tile([P, ROW_TILES, RANGE], F32, name="lse_of_two")
            t["lse"] = larger
            for m in TILES:
                vector(larger[:, m], t["logit_t"][:, m], t["logit_d"][:, m], ALU.max)

        def shares(r):
            t = tiles_of[r]
            ln_larger = work.tile([P, ROW_TILES, RANGE], F32, name="ln_larger")
            t["ln"] = ln_larger
            for m in TILES:
                sigmoid(t["share"], m)
            for m in TILES:
                nc.scalar.activation(out=ln_larger[:, m], in_=t["share"][:, m], func=ACT.Abs, bias=halves[:, 0:1])

        def logarithms(r):
            ln_larger = tiles_of[r]["ln"]
            for m in TILES:
                nc.scalar.activation(out=ln_larger[:, m], in_=ln_larger[:, m], func=ACT.Ln, bias=halves[:, 1:2])

        def first_products(r):
            t = tiles_of[r]
            blend = work.tile([P, ROW_TILES, RANGE], F32, name="blend")
            t["blend"] = blend
            for m in TILES:
                vector(blend[:, m], t["share"][:, m], gap_td[:, m, cols_of(r)], ALU.mult)

        def products(r):
            t = tiles_of[r]
            for m in TILES:
                vector(t["blend"][:, m], t["blend"][:, m], t["share"][:, m], ALU.mult)

        def add_gap(r, gap, m, engine):
            blend = tiles_of[r]["blend"]
            engine.tensor_tensor(out=blend[:, m], in0=blend[:, m], in1=gap[:, m, cols_of(r)], op=ALU.add)

        def gate_l(r):
            tiles_of[r]["logit_l"] = logits_of(GATE_L, r)

        def finish_lse(r):
            t = tiles_of[r]
            for m in TILES:
                vector(t["lse"][:, m], t["lse"][:, m], t["ln"][:, m], ALU.subtract)

        def second_differences(r):
            t = tiles_of[r]
            share = work.tile([P, ROW_TILES, RANGE], F32, name="share")
            t["share"] = share
            for m in TILES:
                vector(share[:, m], t["lse"][:, m], t["logit_l"][:, m], ALU.subtract)

        def second_maxima(r):
            t = tiles_of[r]
            larger = work.tile([P, ROW_TILES, RANGE], F32, name="lse_of_three")
            for m in TILES:
                vector(larger[:, m], t["lse"][:, m], t["logit_l"][:, m], ALU.max)
            t["lse"] = larger

        def logits_of(j, r):
            accs = multiply(j, RANGE * r, RANGE)
            logit = new_logit()
            for m in TILES:
                add_bias(logit, j, r, accs, m)
            return logit

        def last_differences(first_unit, width):
            r = first_unit // RANGE
            inside = slice(first_unit - RANGE * r, first_unit - RANGE * r + width)
            accs = multiply(GATE_I, first_unit, width)
            share = work.tile([P, ROW_TILES, width], F32, name="share")
            for m in TILES:
                vector(share[:, m], tiles_of[r]["lse"][:, m, inside], accs[m][:], ALU.subtract)
            return share

        def last_blend(share, first_unit, width, parts):
            r = first_unit // RANGE
            blend = tiles_of[r]["blend"]
            inside = slice(first_unit - RANGE * r, first_unit - RANGE * r + width)
            for part in parts:
                vector(blend[:, part, inside], blend[:, part, inside], share[:, part], ALU.mult)
            for part in parts:
                vector(
                    blend[:, part, inside],
                    blend[:, part, inside],
                    states[:, GATE_I, part, first_unit : first_unit + width],
                    ALU.add,
                )
            nc.sync.dma_start(out=by_partition(out)[:, :, first_unit : first_unit + width], in_=blend[:, :, inside])

        BOTH = (slice(0, ROW_TILES),)
        HELPER = nc.gpsimd if GPSIMD_ADDS else nc.vector

        accs_t = multiply(GATE_T, 0, RANGE)
        spread_biases()
        tiles_of[0]["logit_t"] = new_logit()
        for m in TILES:
            add_bias(tiles_of[0]["logit_t"], GATE_T, 0, accs_t, m)
        first_differences(0)
        first_maxima(0)
        shares(0)
        logarithms(0)
        first_products(0)
        add_gap(0, gap_dl, 0, HELPER)
        gate_l(0)
        add_gap(0, gap_dl, 1, nc.vector)
        finish_lse(0)
        second_differences(0)
        second_maxima(0)
        shares(0)
        gate_t(1)
        products(0)
        add_gap(0, gap_lh, 0, HELPER)
        first_differences(1)
        add_gap(0, gap_lh, 1, nc.vector)
        first_maxima(1)
        shares(1)
        logarithms(1)
        logarithms(0)
        first_products(1)
        add_gap(1, gap_dl, 0, HELPER)
        gate_l(1)
        add_gap(1, gap_dl, 1, nc.vector)
        finish_lse(1)
        second_differences(1)
        finish_lse(0)
        first_unit, width = LAST_PIECES[0]
        share_0 = last_differences(first_unit, width)
        second_maxima(1)
        shares(1)
        for m in TILES:
            sigmoid(share_0, m)
        logarithms(1)
        products(1)
        for m in TILES:
            add_gap(1, gap_lh, m, nc.vector)
        last_blend(share_0, first_unit, width, TILES)
        finish_lse(1)
        last_shares = [last_differences(first_unit, width) for first_unit, width in LAST_PIECES[1:]]
        for share in last_shares:
            sigmoid(share, BOTH[0])
        for share, (first_unit, width) in zip(last_shares, LAST_PIECES[1:]):
            last_blend(share, first_unit, width, BOTH)
